import numpy as np
import ml_dtypes


def mxq(x, axis, fmt="e4m3"):
    dtype, down = {"e4m3": (ml_dtypes.float8_e4m3fn, 7), "e5m2": (ml_dtypes.float8_e5m2, 14)}[fmt]
    v = np.moveaxis(np.asarray(x, np.float32).astype(ml_dtypes.bfloat16).astype(np.float64), axis, -1)
    blocks = v.reshape(v.shape[:-1] + (-1, 32))
    amax = np.abs(blocks).max(-1, keepdims=True)
    byte = np.maximum(np.where(amax > 0, np.frexp(amax)[1] - 1 + 127, 0) - down, 1)
    scale = np.exp2(byte - 127.0)
    codes = (blocks / scale).astype(np.float32).astype(dtype).astype(np.float64)
    return np.moveaxis((codes * scale).reshape(v.shape), -1, axis)


WIDE = False


def mx_kscale(k):
    if not WIDE:
        return np.ones(k)
    levels = np.array([10, -10, 5, -5, 0])
    a = np.random.permutation(np.resize(levels, k // 512 * 4)).reshape(k // 512, 4)
    idx = np.arange(k)
    return np.exp2(a[idx // 512, idx % 128 // 32])


BF16 = ml_dtypes.bfloat16


def bf(x):
    return np.asarray(x, np.float32).astype(BF16)


def f64(x):
    return np.asarray(x).astype(np.float64)


B, T, H, KD, HD, QB = 4, 1024, 4, 128, 256, 512
D, E = H * KD, H * HD
EPS = 1e-6


def silu(v):
    return v / (1.0 + np.exp(-v))


def setup_inputs():
    s = mx_kscale(D)
    o = np.random.standard_normal((B, T, H, HD)) * 1.2 + np.random.standard_normal((B, T, H, 1)) * 0.5
    return {"x": bf(np.random.standard_normal((B, T, D)) * s),
            "o_ret": bf(o),
            "Wg": bf(np.random.standard_normal((D, E)) / np.sqrt(D) / s[:, None]),
            "bg": bf(np.random.standard_normal(E) * 0.1),
            "Wo": bf(np.random.standard_normal((E, D)) / np.sqrt(E)),
            "bo": bf(np.random.standard_normal(D) * 0.1)}


def reference(x, o_ret, Wg, bg, Wo, bo):
    g = (mxq(f64(x), 2, "e4m3") @ mxq(f64(Wg), 0, "e4m3")) + f64(bg)
    o = f64(o_ret)
    mu = o.mean(-1, keepdims=True)
    var = ((o - mu) ** 2).mean(-1, keepdims=True)
    on = ((o - mu) / np.sqrt(var + EPS)).reshape(B, T, E)
    h = silu(g) * on
    return (mxq(h, 2, "e4m3") @ mxq(f64(Wo), 0, "e4m3")) + f64(bo)

@@ -1,0 +1,273 @@
+from contextlib import ExitStack
+
+import concourse.mybir as mybir
+from concourse.masks import make_identity
+
+F32 = mybir.dt.float32
+BF16 = mybir.dt.bfloat16
+U32 = mybir.dt.uint32
+U8 = mybir.dt.uint8
+FP8X4 = mybir.dt.float8_e4m3fn_x4
+ACT = mybir.ActivationFunctionType
+ALU = mybir.AluOpType
+
+P = 128
+TOKENS = 4096
+D_IN = 512
+E = 1024
+D_OUT = 512
+HEAD = 256
+EPS = 1e-6
+TILES = 4
+ROUND = P * TILES
+ROUNDS = TOKENS // ROUND
+
+FLOPS = 2 * TOKENS * D_IN * E + 2 * TOKENS * E * D_OUT
+
+
+def tile_multiscaleretention_pb_t_kernel(tc, x, o_ret, Wg, bg, Wo, bo, out):
+    nc = tc.nc
+    xf = x.flatten_outer_dims()
+    of = o_ret.rearrange("b t h c -> (b t) (h c)")
+    outf = out.flatten_outer_dims()
+
+    with ExitStack() as ctx:
+        const = ctx.enter_context(tc.tile_pool(name="const", bufs=1))
+        xin = ctx.enter_context(tc.tile_pool(name="xin", bufs=3))
+        oin = ctx.enter_context(tc.tile_pool(name="oin", bufs=4))
+        xq = ctx.enter_context(tc.tile_pool(name="xq", bufs=3))
+        small = ctx.enter_context(tc.tile_pool(name="small", bufs=3))
+        onp = ctx.enter_context(tc.tile_pool(name="onp", bufs=4))
+        sp = ctx.enter_context(tc.tile_pool(name="sp", bufs=3))
+        hp = ctx.enter_context(tc.tile_pool(name="hp", bufs=4))
+        op = ctx.enter_context(tc.tile_pool(name="op", bufs=2))
+        ps_on = ctx.enter_context(tc.psum_pool(name="ps_on", bufs=4))
+        ps_g = ctx.enter_context(tc.psum_pool(name="ps_g", bufs=2))
+        ps_m = ctx.enter_context(tc.psum_pool(name="ps_m", bufs=2))
+
+        x_sb = {}
+        o_sb = {}
+        x_codes = {}
+        x_scales = {}
+        neg_mean = {}
+        rstd = {}
+        on_sb = {}
+        s_sb = {}
+        h_codes = {}
+        h_scales = {}
+
+        def load(j):
+            rows = slice(j * ROUND, (j + 1) * ROUND)
+            xt_in = xin.tile([P, TILES * D_IN], BF16)
+            nc.sync.dma_start(
+                out=xt_in[:].rearrange("p (n k) -> p n k", n=TILES),
+                in_=xf[rows, :].rearrange("(p n) k -> p n k", n=TILES),
+            )
+            x_sb[j] = xt_in
+            ot_in = oin.tile([P, TILES, E], BF16)
+            nc.sync.dma_start(
+                out=ot_in[:], in_=of[rows, :].rearrange("(p n) e -> p n e", n=TILES)
+            )
+            o_sb[j] = ot_in
+
+        ident = const.tile([P, P], F32)
+        make_identity(nc, ident[:])
+
+        wg_raw = const.tile([P, 4, E], BF16)
+        for u in range(2):
+            nc.sync.dma_start(
+                out=wg_raw[:, 2 * u : 2 * u + 2, :],
+                in_=Wg[256 * u : 256 * u + 256, :].rearrange("(p e2) n -> p e2 n", e2=2),
+            )
+        load(0)
+        bg_rows = const.tile([P, P], BF16)
+        nc.vector.memset(bg_rows[:], 0.0)
+        nc.sync.dma_start(out=bg_rows[0:8, :], in_=bg.rearrange("(c p) -> c p", p=P))
+        wo_raw = const.tile([P, 8, D_OUT], BF16)
+        nc.sync.dma_start(out=wo_raw[:], in_=Wo.rearrange("(q p) d -> p q d", p=P))
+        load(1)
+        bo_b = const.tile([P, D_OUT], BF16)
+        nc.sync.dma_start(out=bo_b[:], in_=bo.partition_broadcast(P))
+
+        wg_grp = const.tile([P, 4 * E], BF16, align_bytes=64)
+        nc.vector.tensor_copy(
+            out=wg_grp[:].rearrange("p (c i t) -> p c t i", i=4, t=4),
+            in_=wg_raw[:].rearrange("p t (c i) -> p c t i", i=4),
+        )
+        wg_codes = const.tile([P, E], U32, align_bytes=64)
+        wg_scales = const.tile([P, E], U8, align_bytes=64)
+
+        wo_grp = const.tile([P, 2 * 4 * D_OUT], BF16, align_bytes=64)
+        for g in range(2):
+            nc.scalar.copy(
+                out=wo_grp[:, 2048 * g : 2048 * g + 2048].rearrange(
+                    "p (c i t) -> p c t i", i=4, t=4
+                ),
+                in_=wo_raw[:, 4 * g : 4 * g + 4, :].rearrange("p t (c i) -> p c t i", i=4),
+            )
+        wo_codes = const.tile([P, 2 * D_OUT], U32, align_bytes=64)
+        wo_scales = const.tile([P, 2 * D_OUT], U8, align_bytes=64)
+
+        bg_f32 = const.tile([P, P], F32)
+        nc.vector.tensor_copy(out=bg_f32[:], in_=bg_rows[:])
+        nc.vector.quantize_mx(
+            out=wg_codes[:].bitcast(FP8X4), scales=wg_scales[:], in_=wg_grp[:]
+        )
+        bg_ps = ps_m.tile([P, P], F32, tag="misc")
+        nc.tensor.transpose(bg_ps[:], bg_f32[:], ident[:])
+        bg_col = const.tile([P, 8], F32)
+        nc.vector.tensor_copy(out=bg_col[:], in_=bg_ps[:, 0:8])
+
+        def xprep(j):
+            words = x_sb[j][:].bitcast(F32)
+            x_grp = xq.tile([P, 4 * ROUND], BF16, align_bytes=64)
+            grp_w = x_grp[:].bitcast(F32).rearrange("p (n t u) -> p n t u", n=TILES, u=2)
+            for a in range(2):
+                xt_ps = ps_m.tile([P, 2, 2, P], F32, tag="misc")
+                for n2 in range(2):
+                    for u in range(2):
+                        col = 256 * (2 * a + n2) + 128 * u
+                        nc.tensor.transpose(
+                            xt_ps[:, n2, u, :], words[:, col : col + 128], ident[:]
+                        )
+                nc.scalar.copy(
+                    out=grp_w[:, 2 * a : 2 * a + 2, :, :],
+                    in_=xt_ps[:].rearrange("p n u t -> p n t u"),
+                )
+            xc = xq.tile([P, ROUND], U32, align_bytes=64)
+            xs = xq.tile([P, ROUND], U8, align_bytes=64)
+            nc.vector.quantize_mx(out=xc[:].bitcast(FP8X4), scales=xs[:], in_=x_grp[:])
+            x_codes[j] = xc
+            x_scales[j] = xs
+
+        def stats(j):
+            st = small.tile([P, TILES, 2, 6], F32)
+            for n in range(TILES):
+                for q in range(2):
+                    nc.vector.bn_stats(
+                        out=st[:, n, q, :],
+                        in_=o_sb[j][:, n, 512 * q : 512 * q + 512].rearrange(
+                            "p (h c) -> p c h", h=2
+                        ),
+                    )
+            st3 = st[:].rearrange("p n q (h s) -> p (n q h) s", s=3)
+            var = small.tile([P, 4 * TILES], F32)
+            nc.vector.tensor_scalar(
+                out=var[:],
+                in0=st3[:, :, 2],
+                scalar1=1.0 / HEAD,
+                scalar2=EPS,
+                op0=ALU.mult,
+                op1=ALU.add,
+            )
+            sd = small.tile([P, 4 * TILES], F32)
+            nc.scalar.activation(out=sd[:], in_=var[:], func=ACT.Sqrt)
+            rs = small.tile([P, 4 * TILES], F32)
+            nc.vector.reciprocal(out=rs[:], in_=sd[:])
+            nm = small.tile([P, 4 * TILES], F32)
+            nc.vector.tensor_scalar_mul(out=nm[:], in0=st3[:, :, 1], scalar1=-1.0)
+            rstd[j] = rs
+            neg_mean[j] = nm
+
+        def norm(j, g):
+            on_t = onp.tile([P, TILES, 512], F32)
+            for n in range(TILES):
+                for h2 in range(2):
+                    i = 4 * n + 2 * g + h2
+                    lo = 512 * g + HEAD * h2
+                    nc.gpsimd.tensor_scalar(
+                        out=on_t[:, n, HEAD * h2 : HEAD * h2 + HEAD],
+                        in0=o_sb[j][:, n, lo : lo + HEAD],
+                        scalar1=neg_mean[j][:, i : i + 1],
+                        scalar2=rstd[j][:, i : i + 1],
+                        op0=ALU.add,
+                        op1=ALU.mult,
+                    )
+            on_sb[(j, g)] = on_t
+
+        def gate(j, g):
+            s_t = sp.tile([P, 4, ROUND], F32)
+            for k in range(4):
+                c = 4 * g + k
+                g_ps = ps_g.tile([P, ROUND], F32)
+                nc.tensor.matmul_mx(
+                    out=g_ps[:],
+                    lhsT=wg_codes[:, P * c : P * c + P].bitcast(FP8X4),
+                    lhsT_scale=wg_scales[:, P * c : P * c + P],
+                    rhs=x_codes[j][:].bitcast(FP8X4),
+                    rhs_scale=x_scales[j][:],
+                    start=True,
+                    stop=True,
+                )
+                nc.scalar.activation(
+                    out=s_t[:, k, :],
+                    in_=g_ps[:],
+                    func=ACT.Silu,
+                    bias=bg_col[:, c : c + 1],
+                    scale=1.0,
+                )
+            s_sb[(j, g)] = s_t
+
+        def prod(j, g):
+            h_grp = hp.tile([P, 4 * ROUND], BF16, align_bytes=64)
+            h_view = h_grp[:].rearrange("p (t k) -> p t k", k=4)
+            for n in range(TILES):
+                on_ps = ps_on.tile([P, 4, P], F32)
+                for k in range(4):
+                    nc.tensor.transpose(
+                        on_ps[:, k, :], on_sb[(j, g)][:, n, P * k : P * k + P], ident[:]
+                    )
+                nc.vector.tensor_tensor(
+                    out=h_view[:, P * n : P * n + P, :],
+                    in0=s_sb[(j, g)][:, :, P * n : P * n + P].rearrange("p k t -> p t k"),
+                    in1=on_ps[:].rearrange("p k t -> p t k"),
+                    op=ALU.mult,
+                )
+            hc = hp.tile([P, ROUND], U32, align_bytes=64)
+            hs = hp.tile([P, ROUND], U8, align_bytes=64)
+            nc.vector.quantize_mx(out=hc[:].bitcast(FP8X4), scales=hs[:], in_=h_grp[:])
+            h_codes[(j, g)] = hc
+            h_scales[(j, g)] = hs
+
+        def outp(j):
+            o_t = op.tile([P, TILES, D_OUT], F32)
+            for n in range(TILES):
+                o_ps = ps_m.tile([P, D_OUT], F32, tag="misc")
+                for g in range(2):
+                    nc.tensor.matmul_mx(
+                        out=o_ps[:],
+                        lhsT=h_codes[(j, g)][:, P * n : P * n + P].bitcast(FP8X4),
+                        lhsT_scale=h_scales[(j, g)][:, P * n : P * n + P],
+                        rhs=wo_codes[:, D_OUT * g : D_OUT * g + D_OUT].bitcast(FP8X4),
+                        rhs_scale=wo_scales[:, D_OUT * g : D_OUT * g + D_OUT],
+                        start=(g == 0),
+                        stop=(g == 1),
+                    )
+                nc.vector.tensor_tensor(out=o_t[:, n, :], in0=o_ps[:], in1=bo_b[:], op=ALU.add)
+            nc.sync.dma_start(
+                out=outf[j * ROUND : (j + 1) * ROUND, :].rearrange("(p n) d -> p n d", n=TILES),
+                in_=o_t[:],
+            )
+
+        xprep(0)
+        stats(0)
+        nc.vector.quantize_mx(
+            out=wo_codes[:].bitcast(FP8X4), scales=wo_scales[:], in_=wo_grp[:]
+        )
+        norm(0, 0)
+        norm(0, 1)
+        for j in range(ROUNDS):
+            if j + 2 < ROUNDS:
+                load(j + 2)
+            if j + 1 < ROUNDS:
+                xprep(j + 1)
+                stats(j + 1)
+            gate(j, 0)
+            prod(j, 0)
+            if j + 1 < ROUNDS:
+                norm(j + 1, 0)
+            gate(j, 1)
+            prod(j, 1)
+            if j + 1 < ROUNDS:
+                norm(j + 1, 1)
+            outp(j)

@@ -5,6 +5,7 @@ from concourse.masks import make_identity
 
 F32 = mybir.dt.float32
 BF16 = mybir.dt.bfloat16
+I32 = mybir.dt.int32
 U32 = mybir.dt.uint32
 U8 = mybir.dt.uint8
 FP8X4 = mybir.dt.float8_e4m3fn_x4
@@ -21,6 +22,8 @@ EPS = 1e-6
 TILES = 4
 ROUND = P * TILES
 ROUNDS = TOKENS // ROUND
+SLOTS = 8 * ROUNDS
+RSQRT_MAGIC = 1597463007.0
 
 FLOPS = 2 * TOKENS * D_IN * E + 2 * TOKENS * E * D_OUT
 
@@ -34,240 +37,393 @@ def tile_multiscaleretention_pb_t_kernel(tc, x, o_ret, Wg, bg, Wo, bo, out):
     with ExitStack() as ctx:
         const = ctx.enter_context(tc.tile_pool(name="const", bufs=1))
         xin = ctx.enter_context(tc.tile_pool(name="xin", bufs=3))
-        oin = ctx.enter_context(tc.tile_pool(name="oin", bufs=4))
-        xq = ctx.enter_context(tc.tile_pool(name="xq", bufs=3))
-        small = ctx.enter_context(tc.tile_pool(name="small", bufs=3))
-        onp = ctx.enter_context(tc.tile_pool(name="onp", bufs=4))
+        oin = ctx.enter_context(tc.tile_pool(name="oin", bufs=5))
+        xgp = ctx.enter_context(tc.tile_pool(name="xgp", bufs=2))
+        xcp = ctx.enter_context(tc.tile_pool(name="xcp", bufs=3))
+        small = ctx.enter_context(tc.tile_pool(name="small", bufs=6))
+        onp = ctx.enter_context(tc.tile_pool(name="onp", bufs=3))
         sp = ctx.enter_context(tc.tile_pool(name="sp", bufs=3))
-        hp = ctx.enter_context(tc.tile_pool(name="hp", bufs=4))
-        op = ctx.enter_context(tc.tile_pool(name="op", bufs=2))
-        ps_on = ctx.enter_context(tc.psum_pool(name="ps_on", bufs=4))
+        hgp = ctx.enter_context(tc.tile_pool(name="hgp", bufs=2))
+        hcp = ctx.enter_context(tc.tile_pool(name="hcp", bufs=4))
+        outp = ctx.enter_context(tc.tile_pool(name="outp", bufs=2))
+        ps_on = ctx.enter_context(tc.psum_pool(name="ps_on", bufs=3))
         ps_g = ctx.enter_context(tc.psum_pool(name="ps_g", bufs=2))
-        ps_m = ctx.enter_context(tc.psum_pool(name="ps_m", bufs=2))
+        ps_x = ctx.enter_context(tc.psum_pool(name="ps_x", bufs=1))
+        ps_o = ctx.enter_context(tc.psum_pool(name="ps_o", bufs=2))
+        ctx.enter_context(tc.manual_schedule())
 
         x_sb = {}
         o_sb = {}
+        xt_bank = {}
+        x_grp = {}
         x_codes = {}
         x_scales = {}
-        neg_mean = {}
+        bn_out = {}
+        nm_s = {}
+        m2_s = {}
+        nm_v = {}
+        chain_t = {}
         rstd = {}
         on_sb = {}
+        on_bank = {}
+        g_bank = {}
         s_sb = {}
+        h_grp = {}
         h_codes = {}
         h_scales = {}
+        o_bank = {}
+        o_out = {}
 
-        def load(j):
-            rows = slice(j * ROUND, (j + 1) * ROUND)
+        def load_o(r):
+            ot_in = oin.tile([P, TILES, E], BF16)
+            nc.sync.dma_start(
+                out=ot_in[:],
+                in_=of[r * ROUND : (r + 1) * ROUND, :].rearrange("(p n) e -> p n e", n=TILES),
+            )
+            o_sb[r] = ot_in
+
+        def load_x(r):
             xt_in = xin.tile([P, TILES * D_IN], BF16)
             nc.sync.dma_start(
                 out=xt_in[:].rearrange("p (n k) -> p n k", n=TILES),
-                in_=xf[rows, :].rearrange("(p n) k -> p n k", n=TILES),
+                in_=xf[r * ROUND : (r + 1) * ROUND, :].rearrange("(p n) k -> p n k", n=TILES),
             )
-            x_sb[j] = xt_in
-            ot_in = oin.tile([P, TILES, E], BF16)
-            nc.sync.dma_start(
-                out=ot_in[:], in_=of[rows, :].rearrange("(p n) e -> p n e", n=TILES)
-            )
-            o_sb[j] = ot_in
+            x_sb[r] = xt_in
 
         ident = const.tile([P, P], F32)
         make_identity(nc, ident[:])
-
+        bg_rows = const.tile([P, P], BF16)
+        nc.vector.memset(bg_rows[:], 0.0)
+        nc.sync.dma_start(out=bg_rows[0:8, :], in_=bg.rearrange("(c p) -> c p", p=P))
+        load_o(0)
         wg_raw = const.tile([P, 4, E], BF16)
         for u in range(2):
             nc.sync.dma_start(
                 out=wg_raw[:, 2 * u : 2 * u + 2, :],
                 in_=Wg[256 * u : 256 * u + 256, :].rearrange("(p e2) n -> p e2 n", e2=2),
             )
-        load(0)
-        bg_rows = const.tile([P, P], BF16)
-        nc.vector.memset(bg_rows[:], 0.0)
-        nc.sync.dma_start(out=bg_rows[0:8, :], in_=bg.rearrange("(c p) -> c p", p=P))
         wo_raw = const.tile([P, 8, D_OUT], BF16)
-        nc.sync.dma_start(out=wo_raw[:], in_=Wo.rearrange("(q p) d -> p q d", p=P))
-        load(1)
         bo_b = const.tile([P, D_OUT], BF16)
-        nc.sync.dma_start(out=bo_b[:], in_=bo.partition_broadcast(P))
-
         wg_grp = const.tile([P, 4 * E], BF16, align_bytes=64)
-        nc.vector.tensor_copy(
-            out=wg_grp[:].rearrange("p (c i t) -> p c t i", i=4, t=4),
-            in_=wg_raw[:].rearrange("p t (c i) -> p c t i", i=4),
-        )
         wg_codes = const.tile([P, E], U32, align_bytes=64)
         wg_scales = const.tile([P, E], U8, align_bytes=64)
-
         wo_grp = const.tile([P, 2 * 4 * D_OUT], BF16, align_bytes=64)
-        for g in range(2):
+        wo_codes = const.tile([P, 2 * D_OUT], U32, align_bytes=64)
+        wo_scales = const.tile([P, 2 * D_OUT], U8, align_bytes=64)
+        junk = const.tile([P, HEAD], BF16)
+        bg_f32 = const.tile([P, P], F32)
+        nc.vector.tensor_copy(out=bg_f32[:], in_=bg_rows[:])
+        bg_ps = ps_x.tile([P, P], F32, tag="xt")
+        nc.tensor.transpose(bg_ps[:], bg_f32[:], ident[:])
+        bg_col = const.tile([P, 8], F32)
+        nc.vector.tensor_copy(out=bg_col[:], in_=bg_ps[:, 0:8])
+
+        def regroup_wg():
+            nc.vector.tensor_copy(
+                out=wg_grp[:].rearrange("p (c i t) -> p c t i", i=4, t=4),
+                in_=wg_raw[:].rearrange("p t (c i) -> p c t i", i=4),
+            )
+
+        def quantise_wg():
+            nc.vector.quantize_mx(
+                out=wg_codes[:].bitcast(FP8X4), scales=wg_scales[:], in_=wg_grp[:]
+            )
+
+        def regroup_wo(g):
             nc.scalar.copy(
                 out=wo_grp[:, 2048 * g : 2048 * g + 2048].rearrange(
                     "p (c i t) -> p c t i", i=4, t=4
                 ),
                 in_=wo_raw[:, 4 * g : 4 * g + 4, :].rearrange("p t (c i) -> p c t i", i=4),
             )
-        wo_codes = const.tile([P, 2 * D_OUT], U32, align_bytes=64)
-        wo_scales = const.tile([P, 2 * D_OUT], U8, align_bytes=64)
 
-        bg_f32 = const.tile([P, P], F32)
-        nc.vector.tensor_copy(out=bg_f32[:], in_=bg_rows[:])
-        nc.vector.quantize_mx(
-            out=wg_codes[:].bitcast(FP8X4), scales=wg_scales[:], in_=wg_grp[:]
-        )
-        bg_ps = ps_m.tile([P, P], F32, tag="misc")
-        nc.tensor.transpose(bg_ps[:], bg_f32[:], ident[:])
-        bg_col = const.tile([P, 8], F32)
-        nc.vector.tensor_copy(out=bg_col[:], in_=bg_ps[:, 0:8])
-
-        def xprep(j):
-            words = x_sb[j][:].bitcast(F32)
-            x_grp = xq.tile([P, 4 * ROUND], BF16, align_bytes=64)
-            grp_w = x_grp[:].bitcast(F32).rearrange("p (n t u) -> p n t u", n=TILES, u=2)
-            for a in range(2):
-                xt_ps = ps_m.tile([P, 2, 2, P], F32, tag="misc")
-                for n2 in range(2):
-                    for u in range(2):
-                        col = 256 * (2 * a + n2) + 128 * u
-                        nc.tensor.transpose(
-                            xt_ps[:, n2, u, :], words[:, col : col + 128], ident[:]
-                        )
-                nc.scalar.copy(
-                    out=grp_w[:, 2 * a : 2 * a + 2, :, :],
-                    in_=xt_ps[:].rearrange("p n u t -> p n t u"),
+        def x_flip(r, a, part):
+            if part == 0:
+                xt_ps = ps_x.tile([P, 2, 2, P], F32, tag="xt")
+                xt_bank[(r, a)] = xt_ps
+            words = x_sb[r][:].bitcast(F32)
+            for u in range(2):
+                col = 256 * (2 * a + part) + 128 * u
+                nc.tensor.transpose(
+                    xt_bank[(r, a)][:, part, u, :], words[:, col : col + 128], ident[:]
                 )
-            xc = xq.tile([P, ROUND], U32, align_bytes=64)
-            xs = xq.tile([P, ROUND], U8, align_bytes=64)
-            nc.vector.quantize_mx(out=xc[:].bitcast(FP8X4), scales=xs[:], in_=x_grp[:])
-            x_codes[j] = xc
-            x_scales[j] = xs
 
-        def stats(j):
-            st = small.tile([P, TILES, 2, 6], F32)
-            for n in range(TILES):
-                for q in range(2):
-                    nc.vector.bn_stats(
-                        out=st[:, n, q, :],
-                        in_=o_sb[j][:, n, 512 * q : 512 * q + 512].rearrange(
-                            "p (h c) -> p c h", h=2
-                        ),
-                    )
-            st3 = st[:].rearrange("p n q (h s) -> p (n q h) s", s=3)
-            var = small.tile([P, 4 * TILES], F32)
-            nc.vector.tensor_scalar(
-                out=var[:],
-                in0=st3[:, :, 2],
-                scalar1=1.0 / HEAD,
-                scalar2=EPS,
-                op0=ALU.mult,
-                op1=ALU.add,
+        def x_out(r, a):
+            if a == 0:
+                xg = xgp.tile([P, 4 * ROUND], BF16, align_bytes=64)
+                x_grp[r] = xg
+            grp_w = x_grp[r][:].bitcast(F32).rearrange("p (n t u) -> p n t u", n=TILES, u=2)
+            nc.scalar.copy(
+                out=grp_w[:, 2 * a : 2 * a + 2, :, :],
+                in_=xt_bank[(r, a)][:].rearrange("p n u t -> p n t u"),
             )
-            sd = small.tile([P, 4 * TILES], F32)
-            nc.scalar.activation(out=sd[:], in_=var[:], func=ACT.Sqrt)
-            rs = small.tile([P, 4 * TILES], F32)
-            nc.vector.reciprocal(out=rs[:], in_=sd[:])
-            nm = small.tile([P, 4 * TILES], F32)
-            nc.vector.tensor_scalar_mul(out=nm[:], in0=st3[:, :, 1], scalar1=-1.0)
-            rstd[j] = rs
-            neg_mean[j] = nm
 
-        def norm(j, g):
-            on_t = onp.tile([P, TILES, 512], F32)
-            for n in range(TILES):
-                for h2 in range(2):
-                    i = 4 * n + 2 * g + h2
-                    lo = 512 * g + HEAD * h2
-                    nc.gpsimd.tensor_scalar(
-                        out=on_t[:, n, HEAD * h2 : HEAD * h2 + HEAD],
-                        in0=o_sb[j][:, n, lo : lo + HEAD],
-                        scalar1=neg_mean[j][:, i : i + 1],
-                        scalar2=rstd[j][:, i : i + 1],
-                        op0=ALU.add,
-                        op1=ALU.mult,
+        def x_quant(r):
+            xc = xcp.tile([P, ROUND], U32, align_bytes=64)
+            xs = xcp.tile([P, ROUND], U8, align_bytes=64)
+            nc.vector.quantize_mx(out=xc[:].bitcast(FP8X4), scales=xs[:], in_=x_grp[r][:])
+            x_codes[r] = xc
+            x_scales[r] = xs
+
+        def bn(r, idx):
+            if idx == 0:
+                st = small.tile([P, 2, 2, 6], F32)
+                bn_out[r] = st
+            n = idx // 2
+            q = idx % 2
+            nc.vector.bn_stats(
+                out=bn_out[r][:, n, q, :],
+                in_=o_sb[r][:, n, 512 * q : 512 * q + 512].rearrange("p (h c) -> p c h", h=2),
+            )
+
+        def s_stat(r, step):
+            if step == 0:
+                nms = small.tile([P, 8], F32)
+                m2s = small.tile([P, 8], F32)
+                nm_s[r] = nms
+                m2_s[r] = m2s
+            for e2 in range(2):
+                i = 2 * (step % 4) + e2
+                src = o_sb[r][:, 2 + i // 4, HEAD * (i % 4) : HEAD * (i % 4) + HEAD]
+                if step < 4:
+                    nc.scalar.activation(
+                        out=junk[:],
+                        in_=src,
+                        func=ACT.Copy,
+                        scale=-1.0 / HEAD,
+                        accum_out=nm_s[r][:, i : i + 1],
                     )
-            on_sb[(j, g)] = on_t
+                else:
+                    nc.scalar.activation(
+                        out=junk[:],
+                        in_=src,
+                        func=ACT.Square,
+                        bias=nm_s[r][:, i : i + 1],
+                        scale=1.0,
+                        accum_out=m2_s[r][:, i : i + 1],
+                    )
 
-        def gate(j, g):
-            s_t = sp.tile([P, 4, ROUND], F32)
+        def chain(r, idx):
+            if idx == 0:
+                var = small.tile([P, 16], F32)
+                nmv = small.tile([P, 8], F32)
+                half = small.tile([P, 16], I32)
+                ya = small.tile([P, 16], F32)
+                yb = small.tile([P, 16], F32)
+                sq = small.tile([P, 16], F32)
+                hb = small.tile([P, 16], F32)
+                chain_t[r] = (var, half, ya, yb, sq, hb)
+                nm_v[r] = nmv
+                rstd[r] = yb
+            var, half, ya, yb, sq, hb = chain_t[r]
+            st3 = bn_out[r][:].rearrange("p n q (h s) -> p (n q h) s", s=3)
+            if idx == 0:
+                nc.vector.tensor_scalar(
+                    out=var[:, 0:8], in0=st3[:, :, 2], scalar1=1.0 / HEAD, scalar2=EPS,
+                    op0=ALU.mult, op1=ALU.add,
+                )
+            elif idx == 1:
+                nc.vector.tensor_scalar(
+                    out=var[:, 8:16], in0=m2_s[r][:], scalar1=1.0 / HEAD, scalar2=EPS,
+                    op0=ALU.mult, op1=ALU.add,
+                )
+            elif idx == 2:
+                nc.vector.tensor_scalar_mul(out=nm_v[r][:], in0=st3[:, :, 1], scalar1=-1.0)
+            elif idx == 3:
+                nc.vector.tensor_single_scalar(
+                    out=half[:], in_=var[:].bitcast(I32), scalar=1, op=ALU.logical_shift_right
+                )
+            elif idx == 4:
+                nc.vector.tensor_scalar(
+                    out=ya[:].bitcast(I32), in0=half[:], scalar1=-1.0, scalar2=RSQRT_MAGIC,
+                    op0=ALU.mult, op1=ALU.add,
+                )
+            else:
+                it = (idx - 5) // 3
+                cur = (ya, yb, ya)[it]
+                nxt = (yb, ya, yb)[it]
+                step = (idx - 5) % 3
+                if step == 0:
+                    nc.vector.tensor_tensor(out=sq[:], in0=cur[:], in1=cur[:], op=ALU.mult)
+                elif step == 1:
+                    nc.vector.scalar_tensor_tensor(
+                        out=hb[:], in0=sq[:], scalar=-0.5, in1=var[:], op0=ALU.mult, op1=ALU.mult
+                    )
+                else:
+                    nc.vector.scalar_tensor_tensor(
+                        out=nxt[:], in0=hb[:], scalar=1.5, in1=cur[:], op0=ALU.add, op1=ALU.mult
+                    )
+
+        def norm(sig):
+            hr = sig // 4
+            n = sig % 4
+            r = hr // 2
+            g = hr % 2
+            if n == 0:
+                on_t = onp.tile([P, TILES, 512], F32)
+                on_sb[hr] = on_t
+            for h2 in range(2):
+                i = 4 * n + 2 * g + h2
+                lo = 512 * g + HEAD * h2
+                shift = nm_v[r][:, i : i + 1] if n < 2 else nm_s[r][:, i - 8 : i - 7]
+                nc.gpsimd.tensor_scalar(
+                    out=on_sb[hr][:, n, HEAD * h2 : HEAD * h2 + HEAD],
+                    in0=o_sb[r][:, n, lo : lo + HEAD],
+                    scalar1=shift,
+                    scalar2=rstd[r][:, i : i + 1],
+                    op0=ALU.add,
+                    op1=ALU.mult,
+                )
+
+        def flip(sig):
+            hr = sig // 4
+            n = sig % 4
+            on_ps = ps_on.tile([P, 4, P], F32)
+            on_bank[sig] = on_ps
             for k in range(4):
-                c = 4 * g + k
-                g_ps = ps_g.tile([P, ROUND], F32)
-                nc.tensor.matmul_mx(
-                    out=g_ps[:],
-                    lhsT=wg_codes[:, P * c : P * c + P].bitcast(FP8X4),
-                    lhsT_scale=wg_scales[:, P * c : P * c + P],
-                    rhs=x_codes[j][:].bitcast(FP8X4),
-                    rhs_scale=x_scales[j][:],
-                    start=True,
-                    stop=True,
-                )
-                nc.scalar.activation(
-                    out=s_t[:, k, :],
-                    in_=g_ps[:],
-                    func=ACT.Silu,
-                    bias=bg_col[:, c : c + 1],
-                    scale=1.0,
-                )
-            s_sb[(j, g)] = s_t
+                nc.tensor.transpose(on_ps[:, k, :], on_sb[hr][:, n, P * k : P * k + P], ident[:])
 
-        def prod(j, g):
-            h_grp = hp.tile([P, 4 * ROUND], BF16, align_bytes=64)
-            h_view = h_grp[:].rearrange("p (t k) -> p t k", k=4)
-            for n in range(TILES):
-                on_ps = ps_on.tile([P, 4, P], F32)
-                for k in range(4):
-                    nc.tensor.transpose(
-                        on_ps[:, k, :], on_sb[(j, g)][:, n, P * k : P * k + P], ident[:]
-                    )
-                nc.vector.tensor_tensor(
-                    out=h_view[:, P * n : P * n + P, :],
-                    in0=s_sb[(j, g)][:, :, P * n : P * n + P].rearrange("p k t -> p t k"),
-                    in1=on_ps[:].rearrange("p k t -> p t k"),
-                    op=ALU.mult,
-                )
-            hc = hp.tile([P, ROUND], U32, align_bytes=64)
-            hs = hp.tile([P, ROUND], U8, align_bytes=64)
-            nc.vector.quantize_mx(out=hc[:].bitcast(FP8X4), scales=hs[:], in_=h_grp[:])
-            h_codes[(j, g)] = hc
-            h_scales[(j, g)] = hs
-
-        def outp(j):
-            o_t = op.tile([P, TILES, D_OUT], F32)
-            for n in range(TILES):
-                o_ps = ps_m.tile([P, D_OUT], F32, tag="misc")
-                for g in range(2):
-                    nc.tensor.matmul_mx(
-                        out=o_ps[:],
-                        lhsT=h_codes[(j, g)][:, P * n : P * n + P].bitcast(FP8X4),
-                        lhsT_scale=h_scales[(j, g)][:, P * n : P * n + P],
-                        rhs=wo_codes[:, D_OUT * g : D_OUT * g + D_OUT].bitcast(FP8X4),
-                        rhs_scale=wo_scales[:, D_OUT * g : D_OUT * g + D_OUT],
-                        start=(g == 0),
-                        stop=(g == 1),
-                    )
-                nc.vector.tensor_tensor(out=o_t[:, n, :], in0=o_ps[:], in1=bo_b[:], op=ALU.add)
-            nc.sync.dma_start(
-                out=outf[j * ROUND : (j + 1) * ROUND, :].rearrange("(p n) d -> p n d", n=TILES),
-                in_=o_t[:],
+        def gate_mm(m):
+            r = m // 8
+            c = m % 8
+            g_ps = ps_g.tile([P, ROUND], F32)
+            g_bank[m] = g_ps
+            nc.tensor.matmul_mx(
+                out=g_ps[:],
+                lhsT=wg_codes[:, P * c : P * c + P].bitcast(FP8X4),
+                lhsT_scale=wg_scales[:, P * c : P * c + P],
+                rhs=x_codes[r][:].bitcast(FP8X4),
+                rhs_scale=x_scales[r][:],
+                start=True,
+                stop=True,
             )
 
-        xprep(0)
-        stats(0)
-        nc.vector.quantize_mx(
-            out=wo_codes[:].bitcast(FP8X4), scales=wo_scales[:], in_=wo_grp[:]
-        )
-        norm(0, 0)
-        norm(0, 1)
-        for j in range(ROUNDS):
-            if j + 2 < ROUNDS:
-                load(j + 2)
-            if j + 1 < ROUNDS:
-                xprep(j + 1)
-                stats(j + 1)
-            gate(j, 0)
-            prod(j, 0)
-            if j + 1 < ROUNDS:
-                norm(j + 1, 0)
-            gate(j, 1)
-            prod(j, 1)
-            if j + 1 < ROUNDS:
-                norm(j + 1, 1)
-            outp(j)
+        def gate_act(m):
+            hr = m // 4
+            k = m % 4
+            c = m % 8
+            if k == 0:
+                s_t = sp.tile([P, 4, ROUND], F32)
+                s_sb[hr] = s_t
+            nc.scalar.activation(
+                out=s_sb[hr][:, k, :],
+                in_=g_bank[m][:],
+                func=ACT.Silu,
+                bias=bg_col[:, c : c + 1],
+                scale=1.0,
+            )
+
+        def prod(sig):
+            hr = sig // 4
+            n = sig % 4
+            if n == 0:
+                hg = hgp.tile([P, 4 * ROUND], BF16, align_bytes=64)
+                h_grp[hr] = hg
+            nc.vector.tensor_tensor(
+                out=h_grp[hr][:].rearrange("p (t k) -> p t k", k=4)[:, P * n : P * n + P, :],
+                in0=s_sb[hr][:, :, P * n : P * n + P].rearrange("p k t -> p t k"),
+                in1=on_bank[sig][:].rearrange("p k t -> p t k"),
+                op=ALU.mult,
+            )
+
+        def h_quant(hr):
+            hc = hcp.tile([P, ROUND], U32, align_bytes=64)
+            hs = hcp.tile([P, ROUND], U8, align_bytes=64)
+            nc.vector.quantize_mx(out=hc[:].bitcast(FP8X4), scales=hs[:], in_=h_grp[hr][:])
+            h_codes[hr] = hc
+            h_scales[hr] = hs
+
+        def out_mm(pas):
+            q = pas // 2
+            g = pas % 2
+            hr = 2 * (q // 4) + g
+            n = q % 4
+            if g == 0:
+                o_ps = ps_o.tile([P, D_OUT], F32)
+                o_bank[q] = o_ps
+            nc.tensor.matmul_mx(
+                out=o_bank[q][:],
+                lhsT=h_codes[hr][:, P * n : P * n + P].bitcast(FP8X4),
+                lhsT_scale=h_scales[hr][:, P * n : P * n + P],
+                rhs=wo_codes[:, D_OUT * g : D_OUT * g + D_OUT].bitcast(FP8X4),
+                rhs_scale=wo_scales[:, D_OUT * g : D_OUT * g + D_OUT],
+                start=(g == 0),
+                stop=(g == 1),
+            )
+
+        def out_add(q):
+            r = q // 4
+            n = q % 4
+            if n == 0:
+                o_t = outp.tile([P, TILES, D_OUT], F32)
+                o_out[r] = o_t
+            nc.vector.tensor_tensor(
+                out=o_out[r][:, n, :], in0=o_bank[q][:], in1=bo_b[:], op=ALU.add
+            )
+            rows = outf[r * ROUND : (r + 1) * ROUND, :].rearrange("(p n) d -> p n d", n=TILES)
+            if r == ROUNDS - 1:
+                nc.sync.dma_start(out=rows[:, n, :], in_=o_out[r][:, n, :])
+            elif n == TILES - 1:
+                nc.sync.dma_start(out=rows, in_=o_out[r][:])
+
+        for s in range(-32, SLOTS + 11):
+            r, rem = divmod(s + 32, 8)
+            if rem == 0 and 1 <= r < ROUNDS:
+                load_o(r)
+            r, rem = divmod(s + 29, 8)
+            if rem == 0 and 0 <= r < ROUNDS:
+                load_x(r)
+            if s == -22:
+                nc.sync.dma_start(out=wo_raw[:], in_=Wo.rearrange("(q p) d -> p q d", p=P))
+            if s == -14:
+                nc.sync.dma_start(out=bo_b[:], in_=bo.partition_broadcast(P))
+
+            if 0 <= s + 5 < SLOTS:
+                norm(s + 5)
+
+            if 0 <= s + 2 < SLOTS:
+                flip(s + 2)
+            r, rem = divmod(s + 21, 8)
+            if 0 <= r < ROUNDS and rem in (0, 1, 4, 5):
+                x_flip(r, rem // 4, rem % 4)
+
+            r, rem = divmod(s + 24, 8)
+            if 0 <= r < ROUNDS:
+                s_stat(r, rem)
+            r, rem = divmod(s + 19, 8)
+            if 0 <= r < ROUNDS and rem in (0, 4):
+                x_out(r, rem // 4)
+            if s in (-12, -11):
+                regroup_wo(s + 12)
+
+            if 0 <= s + 6 < SLOTS:
+                gate_mm(s + 6)
+                gate_act(s + 6)
+            if 0 <= s - 10 < SLOTS:
+                out_mm(s - 10)
+
+            if 0 <= s < SLOTS:
+                prod(s)
+            rc, remc = divmod(s + 16, 8)
+            if 0 <= rc < ROUNDS and 2 * remc < 14:
+                chain(rc, 2 * remc)
+            if s >= 4 and s % 4 == 0 and s // 4 - 1 < 2 * ROUNDS:
+                h_quant(s // 4 - 1)
+            if s >= 12 and s % 2 == 0 and (s - 12) // 2 < 4 * ROUNDS:
+                out_add((s - 12) // 2)
+            if 0 <= rc < ROUNDS and 2 * remc + 1 < 14:
+                chain(rc, 2 * remc + 1)
+            r, rem = divmod(s + 24, 8)
+            if 0 <= r < ROUNDS and rem % 2 == 1:
+                bn(r, rem // 2)
+            if s == -19:
+                regroup_wg()
+            if s == -17:
+                quantise_wg()
+            r, rem = divmod(s + 13, 8)
+            if rem == 0 and 0 <= r < ROUNDS:
+                x_quant(r)
+            if s == -4:
+                nc.vector.quantize_mx(
+                    out=wo_codes[:].bitcast(FP8X4), scales=wo_scales[:], in_=wo_grp[:]
+                )

@@ -24,6 +24,8 @@ ROUND = P * TILES
 ROUNDS = TOKENS // ROUND
 SLOTS = 8 * ROUNDS
 RSQRT_MAGIC = 1597463007.0
+S_TILES = (1, 1, 0, 1, 0, 1, 0, 0)
+BN_SLOTS = {3: (1, 2, 3, 5, 6, 7), 4: (0, 1, 2, 3, 4, 5, 6, 7)}
 
 FLOPS = 2 * TOKENS * D_IN * E + 2 * TOKENS * E * D_OUT
 
@@ -61,9 +63,10 @@ def tile_multiscaleretention_pb_t_kernel(tc, x, o_ret, Wg, bg, Wo, bo, out):
         bn_out = {}
         nm_s = {}
         m2_s = {}
-        nm_v = {}
-        chain_t = {}
+        seed_t = {}
+        newton_t = {}
         rstd = {}
+        shift = {}
         on_sb = {}
         on_bank = {}
         g_bank = {}
@@ -95,13 +98,21 @@ def tile_multiscaleretention_pb_t_kernel(tc, x, o_ret, Wg, bg, Wo, bo, out):
         bg_rows = const.tile([P, P], BF16)
         nc.vector.memset(bg_rows[:], 0.0)
         nc.sync.dma_start(out=bg_rows[0:8, :], in_=bg.rearrange("(c p) -> c p", p=P))
-        load_o(0)
         wg_raw = const.tile([P, 4, E], BF16)
-        for u in range(2):
-            nc.sync.dma_start(
-                out=wg_raw[:, 2 * u : 2 * u + 2, :],
-                in_=Wg[256 * u : 256 * u + 256, :].rearrange("(p e2) n -> p e2 n", e2=2),
-            )
+
+        def load_wg(a):
+            for u in range(2):
+                nc.sync.dma_start(
+                    out=wg_raw[:, 2 * u : 2 * u + 2, 512 * a : 512 * a + 512],
+                    in_=Wg[256 * u : 256 * u + 256, 512 * a : 512 * a + 512].rearrange(
+                        "(p e2) n -> p e2 n", e2=2
+                    ),
+                )
+
+        load_o(0)
+        load_wg(0)
+        load_x(0)
+        load_wg(1)
         wo_raw = const.tile([P, 8, D_OUT], BF16)
         bo_b = const.tile([P, D_OUT], BF16)
         wg_grp = const.tile([P, 4 * E], BF16, align_bytes=64)
@@ -118,24 +129,24 @@ def tile_multiscaleretention_pb_t_kernel(tc, x, o_ret, Wg, bg, Wo, bo, out):
         bg_col = const.tile([P, 8], F32)
         nc.vector.tensor_copy(out=bg_col[:], in_=bg_ps[:, 0:8])
 
-        def regroup_wg():
+        def regroup(dst, src):
             nc.vector.tensor_copy(
-                out=wg_grp[:].rearrange("p (c i t) -> p c t i", i=4, t=4),
-                in_=wg_raw[:].rearrange("p t (c i) -> p c t i", i=4),
+                out=dst.rearrange("p (c i t) -> p c t i", i=4, t=4),
+                in_=src.rearrange("p t (c i) -> p c t i", i=4),
             )
 
-        def quantise_wg():
+        def regroup_wg(a):
+            regroup(wg_grp[:, 2048 * a : 2048 * a + 2048], wg_raw[:, :, 512 * a : 512 * a + 512])
+
+        def quantise_wg(a):
             nc.vector.quantize_mx(
-                out=wg_codes[:].bitcast(FP8X4), scales=wg_scales[:], in_=wg_grp[:]
+                out=wg_codes[:, 512 * a : 512 * a + 512].bitcast(FP8X4),
+                scales=wg_scales[:, 512 * a : 512 * a + 512],
+                in_=wg_grp[:, 2048 * a : 2048 * a + 2048],
             )
 
         def regroup_wo(g):
-            nc.scalar.copy(
-                out=wo_grp[:, 2048 * g : 2048 * g + 2048].rearrange(
-                    "p (c i t) -> p c t i", i=4, t=4
-                ),
-                in_=wo_raw[:, 4 * g : 4 * g + 4, :].rearrange("p t (c i) -> p c t i", i=4),
-            )
+            regroup(wo_grp[:, 2048 * g : 2048 * g + 2048], wo_raw[:, 4 * g : 4 * g + 4, :])
 
         def x_flip(r, a, part):
             if part == 0:
@@ -167,7 +178,7 @@ def tile_multiscaleretention_pb_t_kernel(tc, x, o_ret, Wg, bg, Wo, bo, out):
 
         def bn(r, idx):
             if idx == 0:
-                st = small.tile([P, 2, 2, 6], F32)
+                st = small.tile([P, TILES, 2, 6], F32)
                 bn_out[r] = st
             n = idx // 2
             q = idx % 2
@@ -178,81 +189,89 @@ def tile_multiscaleretention_pb_t_kernel(tc, x, o_ret, Wg, bg, Wo, bo, out):
 
         def s_stat(r, step):
             if step == 0:
-                nms = small.tile([P, 8], F32)
-                m2s = small.tile([P, 8], F32)
+                nms = small.tile([P, 4], F32)
+                m2s = small.tile([P, 4], F32)
                 nm_s[r] = nms
                 m2_s[r] = m2s
-            for e2 in range(2):
-                i = 2 * (step % 4) + e2
-                src = o_sb[r][:, 2 + i // 4, HEAD * (i % 4) : HEAD * (i % 4) + HEAD]
-                if step < 4:
-                    nc.scalar.activation(
-                        out=junk[:],
-                        in_=src,
-                        func=ACT.Copy,
-                        scale=-1.0 / HEAD,
-                        accum_out=nm_s[r][:, i : i + 1],
-                    )
-                else:
-                    nc.scalar.activation(
-                        out=junk[:],
-                        in_=src,
-                        func=ACT.Square,
-                        bias=nm_s[r][:, i : i + 1],
-                        scale=1.0,
-                        accum_out=m2_s[r][:, i : i + 1],
-                    )
+            i = step % 4
+            src = o_sb[r][:, TILES - 1, HEAD * i : HEAD * i + HEAD]
+            if step < 4:
+                nc.scalar.activation(
+                    out=junk[:], in_=src, func=ACT.Copy, scale=-1.0 / HEAD,
+                    accum_out=nm_s[r][:, i : i + 1],
+                )
+            else:
+                nc.scalar.activation(
+                    out=junk[:], in_=src, func=ACT.Square, bias=nm_s[r][:, i : i + 1], scale=1.0,
+                    accum_out=m2_s[r][:, i : i + 1],
+                )
 
-        def chain(r, idx):
+        def seed(r):
+            nv = 4 * (TILES - S_TILES[r])
+            var = small.tile([P, 16], F32)
+            half = small.tile([P, 16], I32)
+            y0 = small.tile([P, 16], F32)
+            seed_t[r] = (var, y0)
+            st3 = bn_out[r][:].rearrange("p n q (h s) -> p (n q h) s", s=3)
+            nc.vector.tensor_scalar(
+                out=var[:, 0:nv], in0=st3[:, 0:nv, 2], scalar1=1.0 / HEAD, scalar2=EPS,
+                op0=ALU.mult, op1=ALU.add,
+            )
+            if nv < 16:
+                nc.vector.tensor_scalar(
+                    out=var[:, nv:16], in0=m2_s[r][:], scalar1=1.0 / HEAD, scalar2=EPS,
+                    op0=ALU.mult, op1=ALU.add,
+                )
+            nc.vector.tensor_single_scalar(
+                out=half[:], in_=var[:].bitcast(I32), scalar=1, op=ALU.logical_shift_right
+            )
+            nc.vector.tensor_scalar(
+                out=y0[:].bitcast(I32), in0=half[:], scalar1=-1.0, scalar2=RSQRT_MAGIC,
+                op0=ALU.mult, op1=ALU.add,
+            )
+
+        def newton(r, idx):
+            nv = 4 * (TILES - S_TILES[r])
             if idx == 0:
-                var = small.tile([P, 16], F32)
-                nmv = small.tile([P, 8], F32)
-                half = small.tile([P, 16], I32)
+                nmv = small.tile([P, 16], F32)
                 ya = small.tile([P, 16], F32)
                 yb = small.tile([P, 16], F32)
                 sq = small.tile([P, 16], F32)
-                hb = small.tile([P, 16], F32)
-                chain_t[r] = (var, half, ya, yb, sq, hb)
-                nm_v[r] = nmv
-                rstd[r] = yb
-            var, half, ya, yb, sq, hb = chain_t[r]
-            st3 = bn_out[r][:].rearrange("p n q (h s) -> p (n q h) s", s=3)
+                nb = small.tile([P, 16], F32)
+                newton_t[r] = (nmv, ya, yb, sq)
+                rstd[r] = ya
+                shift[r] = nb
+            nmv, ya, yb, sq = newton_t[r]
+            var, y0 = seed_t[r]
             if idx == 0:
-                nc.vector.tensor_scalar(
-                    out=var[:, 0:8], in0=st3[:, :, 2], scalar1=1.0 / HEAD, scalar2=EPS,
+                st3 = bn_out[r][:].rearrange("p n q (h s) -> p (n q h) s", s=3)
+                nc.gpsimd.tensor_scalar(
+                    out=nmv[:, 0:nv], in0=st3[:, 0:nv, 1], scalar1=-1.0, scalar2=0.0,
                     op0=ALU.mult, op1=ALU.add,
                 )
-            elif idx == 1:
-                nc.vector.tensor_scalar(
-                    out=var[:, 8:16], in0=m2_s[r][:], scalar1=1.0 / HEAD, scalar2=EPS,
-                    op0=ALU.mult, op1=ALU.add,
-                )
-            elif idx == 2:
-                nc.vector.tensor_scalar_mul(out=nm_v[r][:], in0=st3[:, :, 1], scalar1=-1.0)
-            elif idx == 3:
-                nc.vector.tensor_single_scalar(
-                    out=half[:], in_=var[:].bitcast(I32), scalar=1, op=ALU.logical_shift_right
-                )
-            elif idx == 4:
-                nc.vector.tensor_scalar(
-                    out=ya[:].bitcast(I32), in0=half[:], scalar1=-1.0, scalar2=RSQRT_MAGIC,
-                    op0=ALU.mult, op1=ALU.add,
-                )
-            else:
-                it = (idx - 5) // 3
-                cur = (ya, yb, ya)[it]
-                nxt = (yb, ya, yb)[it]
-                step = (idx - 5) % 3
+            elif idx <= 12:
+                it = (idx - 1) // 4
+                cur = (y0, ya, yb)[it]
+                nxt = (ya, yb, ya)[it]
+                step = (idx - 1) % 4
                 if step == 0:
-                    nc.vector.tensor_tensor(out=sq[:], in0=cur[:], in1=cur[:], op=ALU.mult)
+                    nc.gpsimd.tensor_tensor(out=sq[:], in0=cur[:], in1=cur[:], op=ALU.mult)
                 elif step == 1:
-                    nc.vector.scalar_tensor_tensor(
-                        out=hb[:], in0=sq[:], scalar=-0.5, in1=var[:], op0=ALU.mult, op1=ALU.mult
+                    nc.gpsimd.tensor_tensor(out=sq[:], in0=sq[:], in1=var[:], op=ALU.mult)
+                elif step == 2:
+                    nc.gpsimd.tensor_scalar(
+                        out=sq[:], in0=sq[:], scalar1=-0.5, scalar2=1.5, op0=ALU.mult, op1=ALU.add
                     )
                 else:
-                    nc.vector.scalar_tensor_tensor(
-                        out=nxt[:], in0=hb[:], scalar=1.5, in1=cur[:], op0=ALU.add, op1=ALU.mult
-                    )
+                    nc.gpsimd.tensor_tensor(out=nxt[:], in0=cur[:], in1=sq[:], op=ALU.mult)
+            elif idx == 13:
+                nc.gpsimd.tensor_tensor(
+                    out=shift[r][:, 0:nv], in0=nmv[:, 0:nv], in1=ya[:, 0:nv], op=ALU.mult
+                )
+            elif nv < 16:
+                nc.gpsimd.tensor_tensor(
+                    out=shift[r][:, nv:16], in0=nm_s[r][:], in1=ya[:, nv:16], op=ALU.mult
+                )
 
         def norm(sig):
             hr = sig // 4
@@ -265,14 +284,12 @@ def tile_multiscaleretention_pb_t_kernel(tc, x, o_ret, Wg, bg, Wo, bo, out):
             for h2 in range(2):
                 i = 4 * n + 2 * g + h2
                 lo = 512 * g + HEAD * h2
-                shift = nm_v[r][:, i : i + 1] if n < 2 else nm_s[r][:, i - 8 : i - 7]
-                nc.gpsimd.tensor_scalar(
+                nc.scalar.activation(
                     out=on_sb[hr][:, n, HEAD * h2 : HEAD * h2 + HEAD],
-                    in0=o_sb[r][:, n, lo : lo + HEAD],
-                    scalar1=shift,
-                    scalar2=rstd[r][:, i : i + 1],
-                    op0=ALU.add,
-                    op1=ALU.mult,
+                    in_=o_sb[r][:, n, lo : lo + HEAD],
+                    func=ACT.Identity,
+                    bias=shift[r][:, i : i + 1],
+                    scale=rstd[r][:, i : i + 1],
                 )
 
         def flip(sig):
@@ -326,12 +343,19 @@ def tile_multiscaleretention_pb_t_kernel(tc, x, o_ret, Wg, bg, Wo, bo, out):
                 op=ALU.mult,
             )
 
-        def h_quant(hr):
-            hc = hcp.tile([P, ROUND], U32, align_bytes=64)
-            hs = hcp.tile([P, ROUND], U8, align_bytes=64)
-            nc.vector.quantize_mx(out=hc[:].bitcast(FP8X4), scales=hs[:], in_=h_grp[hr][:])
-            h_codes[hr] = hc
-            h_scales[hr] = hs
+        def h_quant(sig):
+            hr = sig // 4
+            n = sig % 4
+            if n == 0:
+                hc = hcp.tile([P, ROUND], U32, align_bytes=64)
+                hs = hcp.tile([P, ROUND], U8, align_bytes=64)
+                h_codes[hr] = hc
+                h_scales[hr] = hs
+            nc.vector.quantize_mx(
+                out=h_codes[hr][:, P * n : P * n + P].bitcast(FP8X4),
+                scales=h_scales[hr][:, P * n : P * n + P],
+                in_=h_grp[hr][:, 4 * P * n : 4 * P * n + 4 * P],
+            )
 
         def out_mm(pas):
             q = pas // 2
@@ -366,64 +390,71 @@ def tile_multiscaleretention_pb_t_kernel(tc, x, o_ret, Wg, bg, Wo, bo, out):
             elif n == TILES - 1:
                 nc.sync.dma_start(out=rows, in_=o_out[r][:])
 
-        for s in range(-32, SLOTS + 11):
-            r, rem = divmod(s + 32, 8)
+        for s in range(-31, SLOTS + 7):
+            r, rem = divmod(s + 30, 8)
             if rem == 0 and 1 <= r < ROUNDS:
                 load_o(r)
-            r, rem = divmod(s + 29, 8)
-            if rem == 0 and 0 <= r < ROUNDS:
+            r, rem = divmod(s + 20, 8)
+            if rem == 0 and 1 <= r < ROUNDS:
                 load_x(r)
-            if s == -22:
+            if s == -16:
                 nc.sync.dma_start(out=wo_raw[:], in_=Wo.rearrange("(q p) d -> p q d", p=P))
-            if s == -14:
+            if s == -6:
                 nc.sync.dma_start(out=bo_b[:], in_=bo.partition_broadcast(P))
 
-            if 0 <= s + 5 < SLOTS:
-                norm(s + 5)
+            r, rem = divmod(s + 12, 8)
+            if 0 <= r < ROUNDS and rem < 5:
+                for idx in range(3 * rem, 3 * rem + 3):
+                    newton(r, idx)
 
             if 0 <= s + 2 < SLOTS:
                 flip(s + 2)
-            r, rem = divmod(s + 21, 8)
-            if 0 <= r < ROUNDS and rem in (0, 1, 4, 5):
-                x_flip(r, rem // 4, rem % 4)
+            r, rem = divmod(s + 14, 8)
+            if 0 <= r < ROUNDS and rem in (0, 1, 3, 4):
+                x_flip(r, rem // 3, rem % 3)
 
-            r, rem = divmod(s + 24, 8)
-            if 0 <= r < ROUNDS:
-                s_stat(r, rem)
-            r, rem = divmod(s + 19, 8)
-            if 0 <= r < ROUNDS and rem in (0, 4):
-                x_out(r, rem // 4)
-            if s in (-12, -11):
-                regroup_wo(s + 12)
+            if 0 <= s + 5 < SLOTS:
+                norm(s + 5)
+            rs, rems = divmod(s + 21, 8)
+            if 0 <= rs < ROUNDS and S_TILES[rs] == 1:
+                s_stat(rs, rems)
+            r, rem = divmod(s + 12, 8)
+            if 0 <= r < ROUNDS and rem in (0, 3):
+                x_out(r, rem // 3)
 
             if 0 <= s + 6 < SLOTS:
                 gate_mm(s + 6)
                 gate_act(s + 6)
-            if 0 <= s - 10 < SLOTS:
-                out_mm(s - 10)
+            if 0 <= s - 6 < SLOTS:
+                out_mm(s - 6)
 
             if 0 <= s < SLOTS:
                 prod(s)
-            rc, remc = divmod(s + 16, 8)
-            if 0 <= rc < ROUNDS and 2 * remc < 14:
-                chain(rc, 2 * remc)
-            if s >= 4 and s % 4 == 0 and s // 4 - 1 < 2 * ROUNDS:
-                h_quant(s // 4 - 1)
-            if s >= 12 and s % 2 == 0 and (s - 12) // 2 < 4 * ROUNDS:
-                out_add((s - 12) // 2)
-            if 0 <= rc < ROUNDS and 2 * remc + 1 < 14:
-                chain(rc, 2 * remc + 1)
-            r, rem = divmod(s + 24, 8)
-            if 0 <= r < ROUNDS and rem % 2 == 1:
-                bn(r, rem // 2)
-            if s == -19:
-                regroup_wg()
-            if s == -17:
-                quantise_wg()
+            if 0 <= s - 1 < SLOTS:
+                h_quant(s - 1)
+            if s >= 8 and s % 2 == 0 and (s - 8) // 2 < 4 * ROUNDS:
+                out_add((s - 8) // 2)
+            if 0 <= rs < ROUNDS:
+                slots = BN_SLOTS[TILES - S_TILES[rs]]
+                if rems in slots:
+                    bn(rs, slots.index(rems))
             r, rem = divmod(s + 13, 8)
             if rem == 0 and 0 <= r < ROUNDS:
+                seed(r)
+            r, rem = divmod(s + 8, 8)
+            if rem == 0 and 0 <= r < ROUNDS:
                 x_quant(r)
-            if s == -4:
+            if s == -17:
+                regroup_wg(0)
+            if s == -12:
+                quantise_wg(0)
+            if s == -11:
+                regroup_wg(1)
+            if s == -9:
+                quantise_wg(1)
+            if s in (-7, -6):
+                regroup_wo(s + 7)
+            if s == -3:
                 nc.vector.quantize_mx(
                     out=wo_codes[:].bitcast(FP8X4), scales=wo_scales[:], in_=wo_grp[:]
                 )

@@ -343,18 +343,16 @@ def tile_multiscaleretention_pb_t_kernel(tc, x, o_ret, Wg, bg, Wo, bo, out):
                 op=ALU.mult,
             )
 
-        def h_quant(sig):
-            hr = sig // 4
-            n = sig % 4
-            if n == 0:
+        def h_quant(hr, pair):
+            if pair == 0:
                 hc = hcp.tile([P, ROUND], U32, align_bytes=64)
                 hs = hcp.tile([P, ROUND], U8, align_bytes=64)
                 h_codes[hr] = hc
                 h_scales[hr] = hs
             nc.vector.quantize_mx(
-                out=h_codes[hr][:, P * n : P * n + P].bitcast(FP8X4),
-                scales=h_scales[hr][:, P * n : P * n + P],
-                in_=h_grp[hr][:, 4 * P * n : 4 * P * n + 4 * P],
+                out=h_codes[hr][:, 2 * P * pair : 2 * P * pair + 2 * P].bitcast(FP8X4),
+                scales=h_scales[hr][:, 2 * P * pair : 2 * P * pair + 2 * P],
+                in_=h_grp[hr][:, 8 * P * pair : 8 * P * pair + 8 * P],
             )
 
         def out_mm(pas):
@@ -390,58 +388,16 @@ def tile_multiscaleretention_pb_t_kernel(tc, x, o_ret, Wg, bg, Wo, bo, out):
             elif n == TILES - 1:
                 nc.sync.dma_start(out=rows, in_=o_out[r][:])
 
-        for s in range(-31, SLOTS + 7):
-            r, rem = divmod(s + 30, 8)
-            if rem == 0 and 1 <= r < ROUNDS:
-                load_o(r)
-            r, rem = divmod(s + 20, 8)
-            if rem == 0 and 1 <= r < ROUNDS:
-                load_x(r)
-            if s == -16:
-                nc.sync.dma_start(out=wo_raw[:], in_=Wo.rearrange("(q p) d -> p q d", p=P))
-            if s == -6:
-                nc.sync.dma_start(out=bo_b[:], in_=bo.partition_broadcast(P))
-
-            r, rem = divmod(s + 12, 8)
-            if 0 <= r < ROUNDS and rem < 5:
-                for idx in range(3 * rem, 3 * rem + 3):
-                    newton(r, idx)
-
-            if 0 <= s + 2 < SLOTS:
-                flip(s + 2)
-            r, rem = divmod(s + 14, 8)
-            if 0 <= r < ROUNDS and rem in (0, 1, 3, 4):
-                x_flip(r, rem // 3, rem % 3)
-
-            if 0 <= s + 5 < SLOTS:
-                norm(s + 5)
+        def vector_sbuf_work(s):
             rs, rems = divmod(s + 21, 8)
-            if 0 <= rs < ROUNDS and S_TILES[rs] == 1:
-                s_stat(rs, rems)
-            r, rem = divmod(s + 12, 8)
-            if 0 <= r < ROUNDS and rem in (0, 3):
-                x_out(r, rem // 3)
-
-            if 0 <= s + 6 < SLOTS:
-                gate_mm(s + 6)
-                gate_act(s + 6)
-            if 0 <= s - 6 < SLOTS:
-                out_mm(s - 6)
-
-            if 0 <= s < SLOTS:
-                prod(s)
-            if 0 <= s - 1 < SLOTS:
-                h_quant(s - 1)
-            if s >= 8 and s % 2 == 0 and (s - 8) // 2 < 4 * ROUNDS:
-                out_add((s - 8) // 2)
             if 0 <= rs < ROUNDS:
                 slots = BN_SLOTS[TILES - S_TILES[rs]]
                 if rems in slots:
                     bn(rs, slots.index(rems))
-            r, rem = divmod(s + 13, 8)
+            r, rem = divmod(s + 12, 8)
             if rem == 0 and 0 <= r < ROUNDS:
                 seed(r)
-            r, rem = divmod(s + 8, 8)
+            r, rem = divmod(s + 10, 8)
             if rem == 0 and 0 <= r < ROUNDS:
                 x_quant(r)
             if s == -17:
@@ -458,3 +414,68 @@ def tile_multiscaleretention_pb_t_kernel(tc, x, o_ret, Wg, bg, Wo, bo, out):
                 nc.vector.quantize_mx(
                     out=wo_codes[:].bitcast(FP8X4), scales=wo_scales[:], in_=wo_grp[:]
                 )
+
+        def scalar_sbuf_work(s):
+            if 0 <= s + 5 < SLOTS:
+                norm(s + 5)
+
+        def scalar_stats(s):
+            rs, rems = divmod(s + 21, 8)
+            if 0 <= rs < ROUNDS and S_TILES[rs] == 1:
+                s_stat(rs, rems)
+
+        def scalar_psum_work(s):
+            if 0 <= s + 6 < SLOTS:
+                gate_act(s + 6)
+
+        def scalar_x_out(s):
+            r, rem = divmod(s + 15, 8)
+            if 0 <= r < ROUNDS and rem in (0, 3):
+                x_out(r, rem // 3)
+
+        for s in range(-32, SLOTS + 10):
+            r, rem = divmod(s + 30, 8)
+            if rem == 0 and 1 <= r < ROUNDS:
+                load_o(r)
+            r, rem = divmod(s + 24, 8)
+            if rem == 0 and 1 <= r < ROUNDS:
+                load_x(r)
+            if s == -16:
+                nc.sync.dma_start(out=wo_raw[:], in_=Wo.rearrange("(q p) d -> p q d", p=P))
+            if s == -6:
+                nc.sync.dma_start(out=bo_b[:], in_=bo.partition_broadcast(P))
+
+            r, rem = divmod(s + 11, 8)
+            if 0 <= r < ROUNDS and rem < 5:
+                for idx in range(3 * rem, 3 * rem + 3):
+                    newton(r, idx)
+
+            if 0 <= s + 2 < SLOTS:
+                flip(s + 2)
+            r, rem = divmod(s + 16, 8)
+            if 0 <= r < ROUNDS and rem in (0, 1, 3, 4):
+                x_flip(r, rem // 3, rem % 3)
+            if 0 <= s + 6 < SLOTS:
+                gate_mm(s + 6)
+            if 0 <= s - 8 < SLOTS:
+                out_mm(s - 8)
+
+            if s % 2 == 1:
+                scalar_sbuf_work(s - 1)
+                scalar_sbuf_work(s)
+                scalar_stats(s - 1)
+                scalar_stats(s)
+                scalar_psum_work(s - 1)
+                scalar_psum_work(s)
+                scalar_x_out(s - 1)
+                scalar_x_out(s)
+            else:
+                if 0 <= s < SLOTS:
+                    prod(s)
+                    prod(s + 1)
+                if s >= 10 and (s - 10) // 2 < 4 * ROUNDS:
+                    out_add((s - 10) // 2)
+                if 0 <= s - 2 < SLOTS:
+                    h_quant((s - 2) // 4, ((s - 2) % 4) // 2)
+                vector_sbuf_work(s)
+                vector_sbuf_work(s + 1)

@@ -24,7 +24,8 @@ ROUND = P * TILES
 ROUNDS = TOKENS // ROUND
 SLOTS = 8 * ROUNDS
 RSQRT_MAGIC = 1597463007.0
-S_TILES = (1, 1, 0, 1, 0, 1, 0, 0)
+S_TILES = (1, 1, 1, 1, 1, 1, 1, 1)
+G_NORM = (1, 3)
 BN_SLOTS = {3: (1, 2, 3, 5, 6, 7), 4: (0, 1, 2, 3, 4, 5, 6, 7)}
 
 FLOPS = 2 * TOKENS * D_IN * E + 2 * TOKENS * E * D_OUT
@@ -39,7 +40,7 @@ def tile_multiscaleretention_pb_t_kernel(tc, x, o_ret, Wg, bg, Wo, bo, out):
     with ExitStack() as ctx:
         const = ctx.enter_context(tc.tile_pool(name="const", bufs=1))
         xin = ctx.enter_context(tc.tile_pool(name="xin", bufs=3))
-        oin = ctx.enter_context(tc.tile_pool(name="oin", bufs=5))
+        oin = ctx.enter_context(tc.tile_pool(name="oin", bufs=6))
         xgp = ctx.enter_context(tc.tile_pool(name="xgp", bufs=2))
         xcp = ctx.enter_context(tc.tile_pool(name="xcp", bufs=3))
         small = ctx.enter_context(tc.tile_pool(name="small", bufs=6))
@@ -278,19 +279,29 @@ def tile_multiscaleretention_pb_t_kernel(tc, x, o_ret, Wg, bg, Wo, bo, out):
             n = sig % 4
             r = hr // 2
             g = hr % 2
-            if n == 0:
+            if hr not in on_sb:
                 on_t = onp.tile([P, TILES, 512], F32)
                 on_sb[hr] = on_t
             for h2 in range(2):
                 i = 4 * n + 2 * g + h2
                 lo = 512 * g + HEAD * h2
-                nc.scalar.activation(
-                    out=on_sb[hr][:, n, HEAD * h2 : HEAD * h2 + HEAD],
-                    in_=o_sb[r][:, n, lo : lo + HEAD],
-                    func=ACT.Identity,
-                    bias=shift[r][:, i : i + 1],
-                    scale=rstd[r][:, i : i + 1],
-                )
+                if n in G_NORM:
+                    nc.gpsimd.tensor_scalar(
+                        out=on_sb[hr][:, n, HEAD * h2 : HEAD * h2 + HEAD],
+                        in0=o_sb[r][:, n, lo : lo + HEAD],
+                        scalar1=rstd[r][:, i : i + 1],
+                        scalar2=shift[r][:, i : i + 1],
+                        op0=ALU.mult,
+                        op1=ALU.add,
+                    )
+                else:
+                    nc.scalar.activation(
+                        out=on_sb[hr][:, n, HEAD * h2 : HEAD * h2 + HEAD],
+                        in_=o_sb[r][:, n, lo : lo + HEAD],
+                        func=ACT.Identity,
+                        bias=shift[r][:, i : i + 1],
+                        scale=rstd[r][:, i : i + 1],
+                    )
 
         def flip(sig):
             hr = sig // 4
@@ -389,12 +400,12 @@ def tile_multiscaleretention_pb_t_kernel(tc, x, o_ret, Wg, bg, Wo, bo, out):
                 nc.sync.dma_start(out=rows, in_=o_out[r][:])
 
         def vector_sbuf_work(s):
-            rs, rems = divmod(s + 21, 8)
+            rs, rems = divmod(s + 25, 8)
             if 0 <= rs < ROUNDS:
                 slots = BN_SLOTS[TILES - S_TILES[rs]]
                 if rems in slots:
                     bn(rs, slots.index(rems))
-            r, rem = divmod(s + 12, 8)
+            r, rem = divmod(s + 16, 8)
             if rem == 0 and 0 <= r < ROUNDS:
                 seed(r)
             r, rem = divmod(s + 10, 8)
@@ -416,11 +427,11 @@ def tile_multiscaleretention_pb_t_kernel(tc, x, o_ret, Wg, bg, Wo, bo, out):
                 )
 
         def scalar_sbuf_work(s):
-            if 0 <= s + 5 < SLOTS:
+            if 0 <= s + 5 < SLOTS and (s + 5) % 4 not in G_NORM:
                 norm(s + 5)
 
         def scalar_stats(s):
-            rs, rems = divmod(s + 21, 8)
+            rs, rems = divmod(s + 25, 8)
             if 0 <= rs < ROUNDS and S_TILES[rs] == 1:
                 s_stat(rs, rems)
 
@@ -434,7 +445,7 @@ def tile_multiscaleretention_pb_t_kernel(tc, x, o_ret, Wg, bg, Wo, bo, out):
                 x_out(r, rem // 3)
 
         for s in range(-32, SLOTS + 10):
-            r, rem = divmod(s + 30, 8)
+            r, rem = divmod(s + 34, 8)
             if rem == 0 and 1 <= r < ROUNDS:
                 load_o(r)
             r, rem = divmod(s + 24, 8)
@@ -445,10 +456,12 @@ def tile_multiscaleretention_pb_t_kernel(tc, x, o_ret, Wg, bg, Wo, bo, out):
             if s == -6:
                 nc.sync.dma_start(out=bo_b[:], in_=bo.partition_broadcast(P))
 
-            r, rem = divmod(s + 11, 8)
+            r, rem = divmod(s + 15, 8)
             if 0 <= r < ROUNDS and rem < 5:
                 for idx in range(3 * rem, 3 * rem + 3):
                     newton(r, idx)
+            if 0 <= s + 9 < SLOTS and (s + 9) % 4 in G_NORM:
+                norm(s + 9)
 
             if 0 <= s + 2 < SLOTS:
                 flip(s + 2)

@@ -348,9 +348,11 @@ def tile_multiscaleretention_pb_t_kernel(tc, x, o_ret, Wg, bg, Wo, bo, out):
                 hg = hgp.tile([P, 4 * ROUND], BF16, align_bytes=64)
                 h_grp[hr] = hg
             nc.vector.tensor_tensor(
-                out=h_grp[hr][:].rearrange("p (t k) -> p t k", k=4)[:, P * n : P * n + P, :],
-                in0=s_sb[hr][:, :, P * n : P * n + P].rearrange("p k t -> p t k"),
-                in1=on_bank[sig][:].rearrange("p k t -> p t k"),
+                out=h_grp[hr][:, 4 * P * n : 4 * P * n + 4 * P].rearrange(
+                    "p (c i k) -> p c k i", i=4, k=4
+                ),
+                in0=s_sb[hr][:, :, P * n : P * n + P].rearrange("p k (c i) -> p c k i", i=4),
+                in1=on_bank[sig][:].rearrange("p k (c i) -> p c k i", i=4),
                 op=ALU.mult,
             )
 

@@ -66,6 +66,7 @@ def tile_multiscaleretention_pb_t_kernel(tc, x, o_ret, Wg, bg, Wo, bo, out):
         m2_s = {}
         seed_t = {}
         newton_t = {}
+        half_var = {}
         rstd = {}
         shift = {}
         on_sb = {}
@@ -80,10 +81,12 @@ def tile_multiscaleretention_pb_t_kernel(tc, x, o_ret, Wg, bg, Wo, bo, out):
 
         def load_o(r):
             ot_in = oin.tile([P, TILES, E], BF16)
-            nc.sync.dma_start(
-                out=ot_in[:],
-                in_=of[r * ROUND : (r + 1) * ROUND, :].rearrange("(p n) e -> p n e", n=TILES),
-            )
+            rows = of[r * ROUND : (r + 1) * ROUND, :].rearrange("(p n) e -> p n e", n=TILES)
+            if r < 2:
+                for n in (0, 3, 1, 2):
+                    nc.sync.dma_start(out=ot_in[:, n, :], in_=rows[:, n, :])
+            else:
+                nc.sync.dma_start(out=ot_in[:], in_=rows)
             o_sb[r] = ot_in
 
         def load_x(r):
@@ -112,8 +115,8 @@ def tile_multiscaleretention_pb_t_kernel(tc, x, o_ret, Wg, bg, Wo, bo, out):
 
         load_o(0)
         load_wg(0)
-        load_x(0)
         load_wg(1)
+        load_x(0)
         wo_raw = const.tile([P, 8, D_OUT], BF16)
         bo_b = const.tile([P, D_OUT], BF16)
         wg_grp = const.tile([P, 4 * E], BF16, align_bytes=64)
@@ -125,10 +128,9 @@ def tile_multiscaleretention_pb_t_kernel(tc, x, o_ret, Wg, bg, Wo, bo, out):
         junk = const.tile([P, HEAD], BF16)
         bg_f32 = const.tile([P, P], F32)
         nc.vector.tensor_copy(out=bg_f32[:], in_=bg_rows[:])
-        bg_ps = ps_x.tile([P, P], F32, tag="xt")
+        bg_ps = ps_o.tile([P, P], F32, tag="o_ps")
         nc.tensor.transpose(bg_ps[:], bg_f32[:], ident[:])
         bg_col = const.tile([P, 8], F32)
-        nc.vector.tensor_copy(out=bg_col[:], in_=bg_ps[:, 0:8])
 
         def regroup(dst, src):
             nc.vector.tensor_copy(
@@ -188,29 +190,33 @@ def tile_multiscaleretention_pb_t_kernel(tc, x, o_ret, Wg, bg, Wo, bo, out):
                 in_=o_sb[r][:, n, 512 * q : 512 * q + 512].rearrange("p (h c) -> p c h", h=2),
             )
 
+        def neg_mean(r):
+            if r not in nm_s:
+                nmv = small.tile([P, 16], F32)
+                nm_s[r] = nmv
+            return nm_s[r]
+
         def s_stat(r, step):
             if step == 0:
-                nms = small.tile([P, 4], F32)
                 m2s = small.tile([P, 4], F32)
-                nm_s[r] = nms
                 m2_s[r] = m2s
             i = step % 4
+            j = 4 * (TILES - 1) + i
             src = o_sb[r][:, TILES - 1, HEAD * i : HEAD * i + HEAD]
             if step < 4:
                 nc.scalar.activation(
                     out=junk[:], in_=src, func=ACT.Copy, scale=-1.0 / HEAD,
-                    accum_out=nm_s[r][:, i : i + 1],
+                    accum_out=neg_mean(r)[:, j : j + 1],
                 )
             else:
                 nc.scalar.activation(
-                    out=junk[:], in_=src, func=ACT.Square, bias=nm_s[r][:, i : i + 1], scale=1.0,
+                    out=junk[:], in_=src, func=ACT.Square, bias=neg_mean(r)[:, j : j + 1], scale=1.0,
                     accum_out=m2_s[r][:, i : i + 1],
                 )
 
         def seed(r):
             nv = 4 * (TILES - S_TILES[r])
             var = small.tile([P, 16], F32)
-            half = small.tile([P, 16], I32)
             y0 = small.tile([P, 16], F32)
             seed_t[r] = (var, y0)
             st3 = bn_out[r][:].rearrange("p n q (h s) -> p (n q h) s", s=3)
@@ -223,56 +229,55 @@ def tile_multiscaleretention_pb_t_kernel(tc, x, o_ret, Wg, bg, Wo, bo, out):
                     out=var[:, nv:16], in0=m2_s[r][:], scalar1=1.0 / HEAD, scalar2=EPS,
                     op0=ALU.mult, op1=ALU.add,
                 )
-            nc.vector.tensor_single_scalar(
-                out=half[:], in_=var[:].bitcast(I32), scalar=1, op=ALU.logical_shift_right
-            )
             nc.vector.tensor_scalar(
-                out=y0[:].bitcast(I32), in0=half[:], scalar1=-1.0, scalar2=RSQRT_MAGIC,
+                out=y0[:].bitcast(I32), in0=var[:].bitcast(I32), scalar1=-0.5, scalar2=RSQRT_MAGIC,
                 op0=ALU.mult, op1=ALU.add,
             )
 
         def newton(r, idx):
             nv = 4 * (TILES - S_TILES[r])
             if idx == 0:
-                nmv = small.tile([P, 16], F32)
                 ya = small.tile([P, 16], F32)
                 yb = small.tile([P, 16], F32)
                 sq = small.tile([P, 16], F32)
+                hy = small.tile([P, 16], F32)
+                ty = small.tile([P, 16], F32)
                 nb = small.tile([P, 16], F32)
-                newton_t[r] = (nmv, ya, yb, sq)
+                newton_t[r] = (ya, yb, sq, hy, ty)
                 rstd[r] = ya
                 shift[r] = nb
-            nmv, ya, yb, sq = newton_t[r]
+            ya, yb, sq, hy, ty = newton_t[r]
             var, y0 = seed_t[r]
             if idx == 0:
+                hv = small.tile([P, 16], F32)
+                half_var[r] = hv
+                nc.gpsimd.tensor_scalar(
+                    out=hv[:], in0=var[:], scalar1=-0.5, scalar2=0.0, op0=ALU.mult, op1=ALU.add
+                )
                 st3 = bn_out[r][:].rearrange("p n q (h s) -> p (n q h) s", s=3)
                 nc.gpsimd.tensor_scalar(
-                    out=nmv[:, 0:nv], in0=st3[:, 0:nv, 1], scalar1=-1.0, scalar2=0.0,
+                    out=neg_mean(r)[:, 0:nv], in0=st3[:, 0:nv, 1], scalar1=-1.0, scalar2=0.0,
                     op0=ALU.mult, op1=ALU.add,
                 )
-            elif idx <= 12:
-                it = (idx - 1) // 4
+            elif idx <= 15:
+                it = (idx - 1) // 5
                 cur = (y0, ya, yb)[it]
                 nxt = (ya, yb, ya)[it]
-                step = (idx - 1) % 4
+                step = (idx - 1) % 5
                 if step == 0:
                     nc.gpsimd.tensor_tensor(out=sq[:], in0=cur[:], in1=cur[:], op=ALU.mult)
                 elif step == 1:
-                    nc.gpsimd.tensor_tensor(out=sq[:], in0=sq[:], in1=var[:], op=ALU.mult)
+                    nc.gpsimd.tensor_tensor(out=hy[:], in0=cur[:], in1=half_var[r][:], op=ALU.mult)
                 elif step == 2:
                     nc.gpsimd.tensor_scalar(
-                        out=sq[:], in0=sq[:], scalar1=-0.5, scalar2=1.5, op0=ALU.mult, op1=ALU.add
+                        out=ty[:], in0=cur[:], scalar1=1.5, scalar2=0.0, op0=ALU.mult, op1=ALU.add
                     )
+                elif step == 3:
+                    nc.gpsimd.tensor_tensor(out=sq[:], in0=sq[:], in1=hy[:], op=ALU.mult)
                 else:
-                    nc.gpsimd.tensor_tensor(out=nxt[:], in0=cur[:], in1=sq[:], op=ALU.mult)
-            elif idx == 13:
-                nc.gpsimd.tensor_tensor(
-                    out=shift[r][:, 0:nv], in0=nmv[:, 0:nv], in1=ya[:, 0:nv], op=ALU.mult
-                )
-            elif nv < 16:
-                nc.gpsimd.tensor_tensor(
-                    out=shift[r][:, nv:16], in0=nm_s[r][:], in1=ya[:, nv:16], op=ALU.mult
-                )
+                    nc.gpsimd.tensor_tensor(out=nxt[:], in0=ty[:], in1=sq[:], op=ALU.add)
+            elif idx == 16:
+                nc.gpsimd.tensor_tensor(out=shift[r][:], in0=neg_mean(r)[:], in1=ya[:], op=ALU.mult)
 
         def norm(sig):
             hr = sig // 4
@@ -392,13 +397,24 @@ def tile_multiscaleretention_pb_t_kernel(tc, x, o_ret, Wg, bg, Wo, bo, out):
             if n == 0:
                 o_t = outp.tile([P, TILES, D_OUT], F32)
                 o_out[r] = o_t
-            nc.vector.tensor_tensor(
-                out=o_out[r][:, n, :], in0=o_bank[q][:], in1=bo_b[:], op=ALU.add
-            )
+            pieces = 2 if q == 4 * ROUNDS - 1 else 1
+            width = D_OUT // pieces
+            for lo in range(0, D_OUT, width):
+                nc.vector.tensor_tensor(
+                    out=o_out[r][:, n, lo : lo + width],
+                    in0=o_bank[q][:, lo : lo + width],
+                    in1=bo_b[:, lo : lo + width],
+                    op=ALU.add,
+                )
+                if r >= ROUNDS - 2:
+                    nc.sync.dma_start(
+                        out=outf[r * ROUND : (r + 1) * ROUND, lo : lo + width].rearrange(
+                            "(p n) d -> p n d", n=TILES
+                        )[:, n, :],
+                        in_=o_out[r][:, n, lo : lo + width],
+                    )
             rows = outf[r * ROUND : (r + 1) * ROUND, :].rearrange("(p n) d -> p n d", n=TILES)
-            if r == ROUNDS - 1:
-                nc.sync.dma_start(out=rows[:, n, :], in_=o_out[r][:, n, :])
-            elif n == TILES - 1:
+            if r < ROUNDS - 2 and n == TILES - 1:
                 nc.sync.dma_start(out=rows, in_=o_out[r][:])
 
         def vector_sbuf_work(s):
@@ -413,17 +429,21 @@ def tile_multiscaleretention_pb_t_kernel(tc, x, o_ret, Wg, bg, Wo, bo, out):
             r, rem = divmod(s + 10, 8)
             if rem == 0 and 0 <= r < ROUNDS:
                 x_quant(r)
+            if s == -23:
+                nc.vector.tensor_copy(out=bg_col[:], in_=bg_ps[:, 0:8])
             if s == -17:
                 regroup_wg(0)
-            if s == -12:
-                quantise_wg(0)
-            if s == -11:
+            if s == -17:
                 regroup_wg(1)
-            if s == -9:
+            if s == -16:
+                quantise_wg(0)
+            if s == -16:
                 quantise_wg(1)
-            if s in (-7, -6):
-                regroup_wo(s + 7)
+            if s == -5:
+                regroup_wo(0)
             if s == -3:
+                regroup_wo(1)
+            if s == 1:
                 nc.vector.quantize_mx(
                     out=wo_codes[:].bitcast(FP8X4), scales=wo_scales[:], in_=wo_grp[:]
                 )
@@ -460,7 +480,7 @@ def tile_multiscaleretention_pb_t_kernel(tc, x, o_ret, Wg, bg, Wo, bo, out):
 
             r, rem = divmod(s + 15, 8)
             if 0 <= r < ROUNDS and rem < 5:
-                for idx in range(3 * rem, 3 * rem + 3):
+                for idx in range(4 * rem, min(4 * rem + 4, 18)):
                     newton(r, idx)
             if 0 <= s + 9 < SLOTS and (s + 9) % 4 in G_NORM:
                 norm(s + 9)

@@ -26,7 +26,7 @@ SLOTS = 8 * ROUNDS
 RSQRT_MAGIC = 1597463007.0
 S_TILES = (1, 1, 1, 1, 1, 1, 1, 1)
 G_NORM = (1, 3)
-BN_SLOTS = {3: (1, 2, 3, 5, 6, 7), 4: (0, 1, 2, 3, 4, 5, 6, 7)}
+BN_SLOTS = {2: (0, 2, 4, 6), 3: (1, 2, 3, 5, 6, 7), 4: (0, 1, 2, 3, 4, 5, 6, 7)}
 
 FLOPS = 2 * TOKENS * D_IN * E + 2 * TOKENS * E * D_OUT
 
@@ -61,9 +61,8 @@ def tile_multiscaleretention_pb_t_kernel(tc, x, o_ret, Wg, bg, Wo, bo, out):
         x_grp = {}
         x_codes = {}
         x_scales = {}
-        bn_out = {}
-        nm_s = {}
-        m2_s = {}
+        stats = {}
+        neg_mean = {}
         seed_t = {}
         newton_t = {}
         half_var = {}
@@ -82,7 +81,7 @@ def tile_multiscaleretention_pb_t_kernel(tc, x, o_ret, Wg, bg, Wo, bo, out):
         def load_o(r):
             ot_in = oin.tile([P, TILES, E], BF16)
             rows = of[r * ROUND : (r + 1) * ROUND, :].rearrange("(p n) e -> p n e", n=TILES)
-            if r < 2:
+            if r < 3:
                 for n in (0, 3, 1, 2):
                     nc.sync.dma_start(out=ot_in[:, n, :], in_=rows[:, n, :])
             else:
@@ -179,63 +178,51 @@ def tile_multiscaleretention_pb_t_kernel(tc, x, o_ret, Wg, bg, Wo, bo, out):
             x_codes[r] = xc
             x_scales[r] = xs
 
+        def open_stats(r):
+            if r not in stats:
+                st = small.tile([P, 16, 3], F32)
+                stats[r] = st
+            return stats[r]
+
         def bn(r, idx):
-            if idx == 0:
-                st = small.tile([P, TILES, 2, 6], F32)
-                bn_out[r] = st
             n = idx // 2
             q = idx % 2
             nc.vector.bn_stats(
-                out=bn_out[r][:, n, q, :],
+                out=open_stats(r)[:, 2 * idx : 2 * idx + 2, :].rearrange("p h s -> p (h s)"),
                 in_=o_sb[r][:, n, 512 * q : 512 * q + 512].rearrange("p (h c) -> p c h", h=2),
             )
 
-        def neg_mean(r):
-            if r not in nm_s:
-                nmv = small.tile([P, 16], F32)
-                nm_s[r] = nmv
-            return nm_s[r]
-
         def s_stat(r, step):
-            if step == 0:
-                m2s = small.tile([P, 4], F32)
-                m2_s[r] = m2s
-            i = step % 4
-            j = 4 * (TILES - 1) + i
-            src = o_sb[r][:, TILES - 1, HEAD * i : HEAD * i + HEAD]
-            if step < 4:
+            t, k = divmod(step, 8)
+            n = TILES - S_TILES[r] + t
+            i = k % 4
+            j = 4 * n + i
+            st = open_stats(r)
+            src = o_sb[r][:, n, HEAD * i : HEAD * i + HEAD]
+            if k < 4:
                 nc.scalar.activation(
-                    out=junk[:], in_=src, func=ACT.Copy, scale=-1.0 / HEAD,
-                    accum_out=neg_mean(r)[:, j : j + 1],
+                    out=junk[:], in_=src, func=ACT.Copy, scale=1.0 / HEAD, accum_out=st[:, j, 1:2]
                 )
             else:
                 nc.scalar.activation(
-                    out=junk[:], in_=src, func=ACT.Square, bias=neg_mean(r)[:, j : j + 1], scale=1.0,
-                    accum_out=m2_s[r][:, i : i + 1],
+                    out=junk[:], in_=src, func=ACT.Square, bias=st[:, j, 1:2], scale=-1.0,
+                    accum_out=st[:, j, 2:3],
                 )
 
         def seed(r):
-            nv = 4 * (TILES - S_TILES[r])
             var = small.tile([P, 16], F32)
             y0 = small.tile([P, 16], F32)
             seed_t[r] = (var, y0)
-            st3 = bn_out[r][:].rearrange("p n q (h s) -> p (n q h) s", s=3)
             nc.vector.tensor_scalar(
-                out=var[:, 0:nv], in0=st3[:, 0:nv, 2], scalar1=1.0 / HEAD, scalar2=EPS,
+                out=var[:], in0=stats[r][:, :, 2], scalar1=1.0 / HEAD, scalar2=EPS,
                 op0=ALU.mult, op1=ALU.add,
             )
-            if nv < 16:
-                nc.vector.tensor_scalar(
-                    out=var[:, nv:16], in0=m2_s[r][:], scalar1=1.0 / HEAD, scalar2=EPS,
-                    op0=ALU.mult, op1=ALU.add,
-                )
             nc.vector.tensor_scalar(
                 out=y0[:].bitcast(I32), in0=var[:].bitcast(I32), scalar1=-0.5, scalar2=RSQRT_MAGIC,
                 op0=ALU.mult, op1=ALU.add,
             )
 
         def newton(r, idx):
-            nv = 4 * (TILES - S_TILES[r])
             if idx == 0:
                 ya = small.tile([P, 16], F32)
                 yb = small.tile([P, 16], F32)
@@ -254,9 +241,10 @@ def tile_multiscaleretention_pb_t_kernel(tc, x, o_ret, Wg, bg, Wo, bo, out):
                 nc.gpsimd.tensor_scalar(
                     out=hv[:], in0=var[:], scalar1=-0.5, scalar2=0.0, op0=ALU.mult, op1=ALU.add
                 )
-                st3 = bn_out[r][:].rearrange("p n q (h s) -> p (n q h) s", s=3)
+                nm = small.tile([P, 16], F32)
+                neg_mean[r] = nm
                 nc.gpsimd.tensor_scalar(
-                    out=neg_mean(r)[:, 0:nv], in0=st3[:, 0:nv, 1], scalar1=-1.0, scalar2=0.0,
+                    out=nm[:], in0=stats[r][:, :, 1], scalar1=-1.0, scalar2=0.0,
                     op0=ALU.mult, op1=ALU.add,
                 )
             elif idx <= 15:
@@ -277,7 +265,7 @@ def tile_multiscaleretention_pb_t_kernel(tc, x, o_ret, Wg, bg, Wo, bo, out):
                 else:
                     nc.gpsimd.tensor_tensor(out=nxt[:], in0=ty[:], in1=sq[:], op=ALU.add)
             elif idx == 16:
-                nc.gpsimd.tensor_tensor(out=shift[r][:], in0=neg_mean(r)[:], in1=ya[:], op=ALU.mult)
+                nc.gpsimd.tensor_tensor(out=shift[r][:], in0=neg_mean[r][:], in1=ya[:], op=ALU.mult)
 
         def norm(sig):
             hr = sig // 4
@@ -321,6 +309,10 @@ def tile_multiscaleretention_pb_t_kernel(tc, x, o_ret, Wg, bg, Wo, bo, out):
             c = m % 8
             g_ps = ps_g.tile([P, ROUND], F32)
             g_bank[m] = g_ps
+            if m < 16:
+                nc.tensor.matmul(
+                    g_ps[:], lhsT=wg_raw[:, 0, 0:P], rhs=wg_raw[:, 0, 0:ROUND], start=True, stop=True
+                )
             nc.tensor.matmul_mx(
                 out=g_ps[:],
                 lhsT=wg_codes[:, P * c : P * c + P].bitcast(FP8X4),
@@ -453,24 +445,25 @@ def tile_multiscaleretention_pb_t_kernel(tc, x, o_ret, Wg, bg, Wo, bo, out):
                 norm(s + 5)
 
         def scalar_stats(s):
-            rs, rems = divmod(s + 25, 8)
-            if 0 <= rs < ROUNDS and S_TILES[rs] == 1:
-                s_stat(rs, rems)
+            rs, rems = divmod(s + 24, 8)
+            if 0 <= rs < ROUNDS and S_TILES[rs]:
+                for step in range(S_TILES[rs] * rems, S_TILES[rs] * rems + S_TILES[rs]):
+                    s_stat(rs, step)
 
         def scalar_psum_work(s):
-            if 0 <= s + 6 < SLOTS:
-                gate_act(s + 6)
+            if 0 <= s + 7 < SLOTS:
+                gate_act(s + 7)
 
         def scalar_x_out(s):
-            r, rem = divmod(s + 15, 8)
-            if 0 <= r < ROUNDS and rem in (0, 3):
-                x_out(r, rem // 3)
+            r, rem = divmod(s + 17, 8)
+            if 0 <= r < ROUNDS and rem in (0, 4):
+                x_out(r, rem // 4)
 
         for s in range(-32, SLOTS + 10):
             r, rem = divmod(s + 34, 8)
             if rem == 0 and 1 <= r < ROUNDS:
                 load_o(r)
-            r, rem = divmod(s + 24, 8)
+            r, rem = divmod(s + 30, 8)
             if rem == 0 and 1 <= r < ROUNDS:
                 load_x(r)
             if s == -16:
@@ -482,25 +475,25 @@ def tile_multiscaleretention_pb_t_kernel(tc, x, o_ret, Wg, bg, Wo, bo, out):
             if 0 <= r < ROUNDS and rem < 5:
                 for idx in range(4 * rem, min(4 * rem + 4, 18)):
                     newton(r, idx)
-            if 0 <= s + 9 < SLOTS and (s + 9) % 4 in G_NORM:
-                norm(s + 9)
+            if 0 <= s + 10 < SLOTS and (s + 10) % 4 in G_NORM:
+                norm(s + 10)
 
             if 0 <= s + 2 < SLOTS:
                 flip(s + 2)
-            r, rem = divmod(s + 16, 8)
-            if 0 <= r < ROUNDS and rem in (0, 1, 3, 4):
-                x_flip(r, rem // 3, rem % 3)
-            if 0 <= s + 6 < SLOTS:
-                gate_mm(s + 6)
+            r, rem = divmod(s + 18, 8)
+            if 0 <= r < ROUNDS and rem in (0, 1, 4, 5):
+                x_flip(r, rem // 4, rem % 4)
+            if 0 <= s + 7 < SLOTS:
+                gate_mm(s + 7)
             if 0 <= s - 8 < SLOTS:
                 out_mm(s - 8)
 
             if s % 2 == 1:
                 scalar_sbuf_work(s - 1)
-                scalar_sbuf_work(s)
                 scalar_stats(s - 1)
-                scalar_stats(s)
                 scalar_psum_work(s - 1)
+                scalar_sbuf_work(s)
+                scalar_stats(s)
                 scalar_psum_work(s)
                 scalar_x_out(s - 1)
                 scalar_x_out(s)

@@ -98,6 +98,8 @@ def tile_multiscaleretention_pb_t_kernel(tc, x, o_ret, Wg, bg, Wo, bo, out):
 
         ident = const.tile([P, P], F32)
         make_identity(nc, ident[:])
+        minus_half = const.tile([P, 16], F32)
+        nc.vector.memset(minus_half[:], -0.5)
         bg_rows = const.tile([P, P], BF16)
         nc.vector.memset(bg_rows[:], 0.0)
         nc.sync.dma_start(out=bg_rows[0:8, :], in_=bg.rearrange("(c p) -> c p", p=P))
@@ -209,63 +211,23 @@ def tile_multiscaleretention_pb_t_kernel(tc, x, o_ret, Wg, bg, Wo, bo, out):
                     accum_out=st[:, j, 2:3],
                 )
 
-        def seed(r):
+        def inverse_deviation(r):
             var = small.tile([P, 16], F32)
-            y0 = small.tile([P, 16], F32)
-            seed_t[r] = (var, y0)
-            nc.vector.tensor_scalar(
+            nm = small.tile([P, 16], F32)
+            rs = small.tile([P, 16], F32)
+            nb = small.tile([P, 16], F32)
+            rstd[r] = rs
+            shift[r] = nb
+            nc.gpsimd.tensor_scalar(
                 out=var[:], in0=stats[r][:, :, 2], scalar1=1.0 / HEAD, scalar2=EPS,
                 op0=ALU.mult, op1=ALU.add,
             )
-            nc.vector.tensor_scalar(
-                out=y0[:].bitcast(I32), in0=var[:].bitcast(I32), scalar1=-0.5, scalar2=RSQRT_MAGIC,
+            nc.gpsimd.tensor_scalar(
+                out=nm[:], in0=stats[r][:, :, 1], scalar1=-1.0, scalar2=0.0,
                 op0=ALU.mult, op1=ALU.add,
             )
-
-        def newton(r, idx):
-            if idx == 0:
-                ya = small.tile([P, 16], F32)
-                yb = small.tile([P, 16], F32)
-                sq = small.tile([P, 16], F32)
-                hy = small.tile([P, 16], F32)
-                ty = small.tile([P, 16], F32)
-                nb = small.tile([P, 16], F32)
-                newton_t[r] = (ya, yb, sq, hy, ty)
-                rstd[r] = ya
-                shift[r] = nb
-            ya, yb, sq, hy, ty = newton_t[r]
-            var, y0 = seed_t[r]
-            if idx == 0:
-                hv = small.tile([P, 16], F32)
-                half_var[r] = hv
-                nc.gpsimd.tensor_scalar(
-                    out=hv[:], in0=var[:], scalar1=-0.5, scalar2=0.0, op0=ALU.mult, op1=ALU.add
-                )
-                nm = small.tile([P, 16], F32)
-                neg_mean[r] = nm
-                nc.gpsimd.tensor_scalar(
-                    out=nm[:], in0=stats[r][:, :, 1], scalar1=-1.0, scalar2=0.0,
-                    op0=ALU.mult, op1=ALU.add,
-                )
-            elif idx <= 15:
-                it = (idx - 1) // 5
-                cur = (y0, ya, yb)[it]
-                nxt = (ya, yb, ya)[it]
-                step = (idx - 1) % 5
-                if step == 0:
-                    nc.gpsimd.tensor_tensor(out=sq[:], in0=cur[:], in1=cur[:], op=ALU.mult)
-                elif step == 1:
-                    nc.gpsimd.tensor_tensor(out=hy[:], in0=cur[:], in1=half_var[r][:], op=ALU.mult)
-                elif step == 2:
-                    nc.gpsimd.tensor_scalar(
-                        out=ty[:], in0=cur[:], scalar1=1.5, scalar2=0.0, op0=ALU.mult, op1=ALU.add
-                    )
-                elif step == 3:
-                    nc.gpsimd.tensor_tensor(out=sq[:], in0=sq[:], in1=hy[:], op=ALU.mult)
-                else:
-                    nc.gpsimd.tensor_tensor(out=nxt[:], in0=ty[:], in1=sq[:], op=ALU.add)
-            elif idx == 16:
-                nc.gpsimd.tensor_tensor(out=shift[r][:], in0=neg_mean[r][:], in1=ya[:], op=ALU.mult)
+            nc.gpsimd.tensor_tensor(out=rs[:], in0=var[:], in1=minus_half[:], op=ALU.pow)
+            nc.gpsimd.tensor_tensor(out=nb[:], in0=nm[:], in1=rs[:], op=ALU.mult)
 
         def norm(sig):
             hr = sig // 4
@@ -371,7 +333,10 @@ def tile_multiscaleretention_pb_t_kernel(tc, x, o_ret, Wg, bg, Wo, bo, out):
             hr = 2 * (q // 4) + g
             n = q % 4
             if g == 0:
-                o_ps = ps_o.tile([P, D_OUT], F32)
+                if q < 4 * ROUNDS - 2:
+                    o_ps = ps_o.tile([P, D_OUT], F32, tag="o_ps")
+                else:
+                    o_ps = ps_g.tile([P, D_OUT], F32, tag="g_ps")
                 o_bank[q] = o_ps
             nc.tensor.matmul_mx(
                 out=o_bank[q][:],
@@ -415,9 +380,6 @@ def tile_multiscaleretention_pb_t_kernel(tc, x, o_ret, Wg, bg, Wo, bo, out):
                 slots = BN_SLOTS[TILES - S_TILES[rs]]
                 if rems in slots:
                     bn(rs, slots.index(rems))
-            r, rem = divmod(s + 16, 8)
-            if rem == 0 and 0 <= r < ROUNDS:
-                seed(r)
             r, rem = divmod(s + 10, 8)
             if rem == 0 and 0 <= r < ROUNDS:
                 x_quant(r)
@@ -472,9 +434,8 @@ def tile_multiscaleretention_pb_t_kernel(tc, x, o_ret, Wg, bg, Wo, bo, out):
                 nc.sync.dma_start(out=bo_b[:], in_=bo.partition_broadcast(P))
 
             r, rem = divmod(s + 15, 8)
-            if 0 <= r < ROUNDS and rem < 5:
-                for idx in range(4 * rem, min(4 * rem + 4, 18)):
-                    newton(r, idx)
+            if rem == 0 and 0 <= r < ROUNDS:
+                inverse_deviation(r)
             if 0 <= s + 10 < SLOTS and (s + 10) % 4 in G_NORM:
                 norm(s + 10)
 

@@ -81,7 +81,7 @@ def tile_multiscaleretention_pb_t_kernel(tc, x, o_ret, Wg, bg, Wo, bo, out):
         def load_o(r):
             ot_in = oin.tile([P, TILES, E], BF16)
             rows = of[r * ROUND : (r + 1) * ROUND, :].rearrange("(p n) e -> p n e", n=TILES)
-            if r < 3:
+            if r < 4:
                 for n in (0, 3, 1, 2):
                     nc.sync.dma_start(out=ot_in[:, n, :], in_=rows[:, n, :])
             else:
@@ -375,7 +375,7 @@ def tile_multiscaleretention_pb_t_kernel(tc, x, o_ret, Wg, bg, Wo, bo, out):
                 nc.sync.dma_start(out=rows, in_=o_out[r][:])
 
         def vector_sbuf_work(s):
-            rs, rems = divmod(s + 25, 8)
+            rs, rems = divmod(s + 27, 8)
             if 0 <= rs < ROUNDS:
                 slots = BN_SLOTS[TILES - S_TILES[rs]]
                 if rems in slots:
@@ -385,26 +385,26 @@ def tile_multiscaleretention_pb_t_kernel(tc, x, o_ret, Wg, bg, Wo, bo, out):
                 x_quant(r)
             if s == -23:
                 nc.vector.tensor_copy(out=bg_col[:], in_=bg_ps[:, 0:8])
-            if s == -17:
+            if s == -19:
                 regroup_wg(0)
-            if s == -17:
+            if s == -19:
                 regroup_wg(1)
-            if s == -16:
+            if s == -18:
                 quantise_wg(0)
-            if s == -16:
+            if s == -10:
                 quantise_wg(1)
-            if s == -5:
-                regroup_wo(0)
             if s == -3:
+                regroup_wo(0)
+            if s == 0:
                 regroup_wo(1)
-            if s == 1:
+            if s == 2:
                 nc.vector.quantize_mx(
                     out=wo_codes[:].bitcast(FP8X4), scales=wo_scales[:], in_=wo_grp[:]
                 )
 
         def scalar_sbuf_work(s):
-            if 0 <= s + 5 < SLOTS and (s + 5) % 4 not in G_NORM:
-                norm(s + 5)
+            if 0 <= s + 4 < SLOTS and (s + 4) % 4 not in G_NORM:
+                norm(s + 4)
 
         def scalar_stats(s):
             rs, rems = divmod(s + 24, 8)
@@ -421,8 +421,8 @@ def tile_multiscaleretention_pb_t_kernel(tc, x, o_ret, Wg, bg, Wo, bo, out):
             if 0 <= r < ROUNDS and rem in (0, 4):
                 x_out(r, rem // 4)
 
-        for s in range(-32, SLOTS + 10):
-            r, rem = divmod(s + 34, 8)
+        for s in range(-34, SLOTS + 10):
+            r, rem = divmod(s + 36, 8)
             if rem == 0 and 1 <= r < ROUNDS:
                 load_o(r)
             r, rem = divmod(s + 30, 8)
@@ -436,13 +436,13 @@ def tile_multiscaleretention_pb_t_kernel(tc, x, o_ret, Wg, bg, Wo, bo, out):
             r, rem = divmod(s + 15, 8)
             if rem == 0 and 0 <= r < ROUNDS:
                 inverse_deviation(r)
-            if 0 <= s + 10 < SLOTS and (s + 10) % 4 in G_NORM:
-                norm(s + 10)
+            if 0 <= s + 12 < SLOTS and (s + 12) % 4 in G_NORM:
+                norm(s + 12)
 
             if 0 <= s + 2 < SLOTS:
                 flip(s + 2)
             r, rem = divmod(s + 18, 8)
-            if 0 <= r < ROUNDS and rem in (0, 1, 4, 5):
+            if 0 <= r < ROUNDS and rem in (0, 1, 4, 4 + 1):
                 x_flip(r, rem // 4, rem % 4)
             if 0 <= s + 7 < SLOTS:
                 gate_mm(s + 7)

from contextlib import ExitStack

import concourse.mybir as mybir
from concourse.masks import make_identity

F32 = mybir.dt.float32
BF16 = mybir.dt.bfloat16
I32 = mybir.dt.int32
U32 = mybir.dt.uint32
U8 = mybir.dt.uint8
FP8X4 = mybir.dt.float8_e4m3fn_x4
ACT = mybir.ActivationFunctionType
ALU = mybir.AluOpType

P = 128
TOKENS = 4096
D_IN = 512
E = 1024
D_OUT = 512
HEAD = 256
EPS = 1e-6
TILES = 4
ROUND = P * TILES
ROUNDS = TOKENS // ROUND
SLOTS = 8 * ROUNDS
RSQRT_MAGIC = 1597463007.0
S_TILES = (1, 1, 1, 1, 1, 1, 1, 1)
G_NORM = (1, 3)
BN_SLOTS = {2: (0, 2, 4, 6), 3: (1, 2, 3, 5, 6, 7), 4: (0, 1, 2, 3, 4, 5, 6, 7)}

FLOPS = 2 * TOKENS * D_IN * E + 2 * TOKENS * E * D_OUT


def tile_multiscaleretention_pb_t_kernel(tc, x, o_ret, Wg, bg, Wo, bo, out):
    nc = tc.nc
    xf = x.flatten_outer_dims()
    of = o_ret.rearrange("b t h c -> (b t) (h c)")
    outf = out.flatten_outer_dims()

    with ExitStack() as ctx:
        const = ctx.enter_context(tc.tile_pool(name="const", bufs=1))
        xin = ctx.enter_context(tc.tile_pool(name="xin", bufs=3))
        oin = ctx.enter_context(tc.tile_pool(name="oin", bufs=6))
        xgp = ctx.enter_context(tc.tile_pool(name="xgp", bufs=2))
        xcp = ctx.enter_context(tc.tile_pool(name="xcp", bufs=3))
        small = ctx.enter_context(tc.tile_pool(name="small", bufs=6))
        onp = ctx.enter_context(tc.tile_pool(name="onp", bufs=3))
        sp = ctx.enter_context(tc.tile_pool(name="sp", bufs=3))
        hgp = ctx.enter_context(tc.tile_pool(name="hgp", bufs=2))
        hcp = ctx.enter_context(tc.tile_pool(name="hcp", bufs=4))
        outp = ctx.enter_context(tc.tile_pool(name="outp", bufs=2))
        ps_on = ctx.enter_context(tc.psum_pool(name="ps_on", bufs=3))
        ps_g = ctx.enter_context(tc.psum_pool(name="ps_g", bufs=2))
        ps_x = ctx.enter_context(tc.psum_pool(name="ps_x", bufs=1))
        ps_o = ctx.enter_context(tc.psum_pool(name="ps_o", bufs=2))
        ctx.enter_context(tc.manual_schedule())

        x_sb = {}
        o_sb = {}
        xt_bank = {}
        x_grp = {}
        x_codes = {}
        x_scales = {}
        stats = {}
        neg_mean = {}
        seed_t = {}
        newton_t = {}
        half_var = {}
        rstd = {}
        shift = {}
        on_sb = {}
        on_bank = {}
        g_bank = {}
        s_sb = {}
        h_grp = {}
        h_codes = {}
        h_scales = {}
        o_bank = {}
        o_out = {}

        def load_o(r):
            ot_in = oin.tile([P, TILES, E], BF16)
            rows = of[r * ROUND : (r + 1) * ROUND, :].rearrange("(p n) e -> p n e", n=TILES)
            if r < 4:
                for n in (0, 3, 1, 2):
                    nc.sync.dma_start(out=ot_in[:, n, :], in_=rows[:, n, :])
            else:
                nc.sync.dma_start(out=ot_in[:], in_=rows)
            o_sb[r] = ot_in

        def load_x(r):
            xt_in = xin.tile([P, TILES * D_IN], BF16)
            nc.sync.dma_start(
                out=xt_in[:].rearrange("p (n k) -> p n k", n=TILES),
                in_=xf[r * ROUND : (r + 1) * ROUND, :].rearrange("(p n) k -> p n k", n=TILES),
            )
            x_sb[r] = xt_in

        ident = const.tile([P, P], F32)
        make_identity(nc, ident[:])
        minus_half = const.tile([P, 16], F32)
        nc.vector.memset(minus_half[:], -0.5)
        bg_rows = const.tile([P, P], BF16)
        nc.vector.memset(bg_rows[:], 0.0)
        nc.sync.dma_start(out=bg_rows[0:8, :], in_=bg.rearrange("(c p) -> c p", p=P))
        wg_raw = const.tile([P, 4, E], BF16)

        def load_wg(a):
            for u in range(2):
                nc.sync.dma_start(
                    out=wg_raw[:, 2 * u : 2 * u + 2, 512 * a : 512 * a + 512],
                    in_=Wg[256 * u : 256 * u + 256, 512 * a : 512 * a + 512].rearrange(
                        "(p e2) n -> p e2 n", e2=2
                    ),
                )

        load_o(0)
        load_wg(0)
        load_wg(1)
        load_x(0)
        wo_raw = const.tile([P, 8, D_OUT], BF16)
        bo_b = const.tile([P, D_OUT], BF16)
        wg_grp = const.tile([P, 4 * E], BF16, align_bytes=64)
        wg_codes = const.tile([P, E], U32, align_bytes=64)
        wg_scales = const.tile([P, E], U8, align_bytes=64)
        wo_grp = const.tile([P, 2 * 4 * D_OUT], BF16, align_bytes=64)
        wo_codes = const.tile([P, 2 * D_OUT], U32, align_bytes=64)
        wo_scales = const.tile([P, 2 * D_OUT], U8, align_bytes=64)
        junk = const.tile([P, HEAD], BF16)
        bg_f32 = const.tile([P, P], F32)
        nc.vector.tensor_copy(out=bg_f32[:], in_=bg_rows[:])
        bg_ps = ps_o.tile([P, P], F32, tag="o_ps")
        nc.tensor.transpose(bg_ps[:], bg_f32[:], ident[:])
        bg_col = const.tile([P, 8], F32)

        def regroup(dst, src):
            nc.vector.tensor_copy(
                out=dst.rearrange("p (c i t) -> p c t i", i=4, t=4),
                in_=src.rearrange("p t (c i) -> p c t i", i=4),
            )

        def regroup_wg(a):
            regroup(wg_grp[:, 2048 * a : 2048 * a + 2048], wg_raw[:, :, 512 * a : 512 * a + 512])

        def quantise_wg(a):
            nc.vector.quantize_mx(
                out=wg_codes[:, 512 * a : 512 * a + 512].bitcast(FP8X4),
                scales=wg_scales[:, 512 * a : 512 * a + 512],
                in_=wg_grp[:, 2048 * a : 2048 * a + 2048],
            )

        def regroup_wo(g):
            regroup(wo_grp[:, 2048 * g : 2048 * g + 2048], wo_raw[:, 4 * g : 4 * g + 4, :])

        def x_flip(r, a, part):
            if part == 0:
                xt_ps = ps_x.tile([P, 2, 2, P], F32, tag="xt")
                xt_bank[(r, a)] = xt_ps
            words = x_sb[r][:].bitcast(F32)
            for u in range(2):
                col = 256 * (2 * a + part) + 128 * u
                nc.tensor.transpose(
                    xt_bank[(r, a)][:, part, u, :], words[:, col : col + 128], ident[:]
                )

        def x_out(r, a):
            if a == 0:
                xg = xgp.tile([P, 4 * ROUND], BF16, align_bytes=64)
                x_grp[r] = xg
            grp_w = x_grp[r][:].bitcast(F32).rearrange("p (n t u) -> p n t u", n=TILES, u=2)
            nc.scalar.copy(
                out=grp_w[:, 2 * a : 2 * a + 2, :, :],
                in_=xt_bank[(r, a)][:].rearrange("p n u t -> p n t u"),
            )

        def x_quant(r):
            xc = xcp.tile([P, ROUND], U32, align_bytes=64)
            xs = xcp.tile([P, ROUND], U8, align_bytes=64)
            nc.vector.quantize_mx(out=xc[:].bitcast(FP8X4), scales=xs[:], in_=x_grp[r][:])
            x_codes[r] = xc
            x_scales[r] = xs

        def open_stats(r):
            if r not in stats:
                st = small.tile([P, 16, 3], F32)
                stats[r] = st
            return stats[r]

        def bn(r, idx):
            n = idx // 2
            q = idx % 2
            nc.vector.bn_stats(
                out=open_stats(r)[:, 2 * idx : 2 * idx + 2, :].rearrange("p h s -> p (h s)"),
                in_=o_sb[r][:, n, 512 * q : 512 * q + 512].rearrange("p (h c) -> p c h", h=2),
            )

        def s_stat(r, step):
            t, k = divmod(step, 8)
            n = TILES - S_TILES[r] + t
            i = k % 4
            j = 4 * n + i
            st = open_stats(r)
            src = o_sb[r][:, n, HEAD * i : HEAD * i + HEAD]
            if k < 4:
                nc.scalar.activation(
                    out=junk[:], in_=src, func=ACT.Copy, scale=1.0 / HEAD, accum_out=st[:, j, 1:2]
                )
            else:
                nc.scalar.activation(
                    out=junk[:], in_=src, func=ACT.Square, bias=st[:, j, 1:2], scale=-1.0,
                    accum_out=st[:, j, 2:3],
                )

        def inverse_deviation(r):
            var = small.tile([P, 16], F32)
            nm = small.tile([P, 16], F32)
            rs = small.tile([P, 16], F32)
            nb = small.tile([P, 16], F32)
            rstd[r] = rs
            shift[r] = nb
            nc.gpsimd.tensor_scalar(
                out=var[:], in0=stats[r][:, :, 2], scalar1=1.0 / HEAD, scalar2=EPS,
                op0=ALU.mult, op1=ALU.add,
            )
            nc.gpsimd.tensor_scalar(
                out=nm[:], in0=stats[r][:, :, 1], scalar1=-1.0, scalar2=0.0,
                op0=ALU.mult, op1=ALU.add,
            )
            nc.gpsimd.tensor_tensor(out=rs[:], in0=var[:], in1=minus_half[:], op=ALU.pow)
            nc.gpsimd.tensor_tensor(out=nb[:], in0=nm[:], in1=rs[:], op=ALU.mult)

        def norm(sig):
            hr = sig // 4
            n = sig % 4
            r = hr // 2
            g = hr % 2
            if hr not in on_sb:
                on_t = onp.tile([P, TILES, 512], F32)
                on_sb[hr] = on_t
            for h2 in range(2):
                i = 4 * n + 2 * g + h2
                lo = 512 * g + HEAD * h2
                if n in G_NORM:
                    nc.gpsimd.tensor_scalar(
                        out=on_sb[hr][:, n, HEAD * h2 : HEAD * h2 + HEAD],
                        in0=o_sb[r][:, n, lo : lo + HEAD],
                        scalar1=rstd[r][:, i : i + 1],
                        scalar2=shift[r][:, i : i + 1],
                        op0=ALU.mult,
                        op1=ALU.add,
                    )
                else:
                    nc.scalar.activation(
                        out=on_sb[hr][:, n, HEAD * h2 : HEAD * h2 + HEAD],
                        in_=o_sb[r][:, n, lo : lo + HEAD],
                        func=ACT.Identity,
                        bias=shift[r][:, i : i + 1],
                        scale=rstd[r][:, i : i + 1],
                    )

        def flip(sig):
            hr = sig // 4
            n = sig % 4
            on_ps = ps_on.tile([P, 4, P], F32)
            on_bank[sig] = on_ps
            for k in range(4):
                nc.tensor.transpose(on_ps[:, k, :], on_sb[hr][:, n, P * k : P * k + P], ident[:])

        def gate_mm(m):
            r = m // 8
            c = m % 8
            g_ps = ps_g.tile([P, ROUND], F32)
            g_bank[m] = g_ps
            if m < 16:
                nc.tensor.matmul(
                    g_ps[:], lhsT=wg_raw[:, 0, 0:P], rhs=wg_raw[:, 0, 0:ROUND], start=True, stop=True
                )
            nc.tensor.matmul_mx(
                out=g_ps[:],
                lhsT=wg_codes[:, P * c : P * c + P].bitcast(FP8X4),
                lhsT_scale=wg_scales[:, P * c : P * c + P],
                rhs=x_codes[r][:].bitcast(FP8X4),
                rhs_scale=x_scales[r][:],
                start=True,
                stop=True,
            )

        def gate_act(m):
            hr = m // 4
            k = m % 4
            c = m % 8
            if k == 0:
                s_t = sp.tile([P, 4, ROUND], F32)
                s_sb[hr] = s_t
            nc.scalar.activation(
                out=s_sb[hr][:, k, :],
                in_=g_bank[m][:],
                func=ACT.Silu,
                bias=bg_col[:, c : c + 1],
                scale=1.0,
            )

        def prod(sig):
            hr = sig // 4
            n = sig % 4
            if n == 0:
                hg = hgp.tile([P, 4 * ROUND], BF16, align_bytes=64)
                h_grp[hr] = hg
            nc.vector.tensor_tensor(
                out=h_grp[hr][:, 4 * P * n : 4 * P * n + 4 * P].rearrange(
                    "p (c i k) -> p c k i", i=4, k=4
                ),
                in0=s_sb[hr][:, :, P * n : P * n + P].rearrange("p k (c i) -> p c k i", i=4),
                in1=on_bank[sig][:].rearrange("p k (c i) -> p c k i", i=4),
                op=ALU.mult,
            )

        def h_quant(hr, pair):
            if pair == 0:
                hc = hcp.tile([P, ROUND], U32, align_bytes=64)
                hs = hcp.tile([P, ROUND], U8, align_bytes=64)
                h_codes[hr] = hc
                h_scales[hr] = hs
            nc.vector.quantize_mx(
                out=h_codes[hr][:, 2 * P * pair : 2 * P * pair + 2 * P].bitcast(FP8X4),
                scales=h_scales[hr][:, 2 * P * pair : 2 * P * pair + 2 * P],
                in_=h_grp[hr][:, 8 * P * pair : 8 * P * pair + 8 * P],
            )

        def out_mm(pas):
            q = pas // 2
            g = pas % 2
            hr = 2 * (q // 4) + g
            n = q % 4
            if g == 0:
                if q < 4 * ROUNDS - 2:
                    o_ps = ps_o.tile([P, D_OUT], F32, tag="o_ps")
                else:
                    o_ps = ps_g.tile([P, D_OUT], F32, tag="g_ps")
                o_bank[q] = o_ps
            nc.tensor.matmul_mx(
                out=o_bank[q][:],
                lhsT=h_codes[hr][:, P * n : P * n + P].bitcast(FP8X4),
                lhsT_scale=h_scales[hr][:, P * n : P * n + P],
                rhs=wo_codes[:, D_OUT * g : D_OUT * g + D_OUT].bitcast(FP8X4),
                rhs_scale=wo_scales[:, D_OUT * g : D_OUT * g + D_OUT],
                start=(g == 0),
                stop=(g == 1),
            )

        def out_add(q):
            r = q // 4
            n = q % 4
            if n == 0:
                o_t = outp.tile([P, TILES, D_OUT], F32)
                o_out[r] = o_t
            pieces = 2 if q == 4 * ROUNDS - 1 else 1
            width = D_OUT // pieces
            for lo in range(0, D_OUT, width):
                nc.vector.tensor_tensor(
                    out=o_out[r][:, n, lo : lo + width],
                    in0=o_bank[q][:, lo : lo + width],
                    in1=bo_b[:, lo : lo + width],
                    op=ALU.add,
                )
                if r >= ROUNDS - 2:
                    nc.sync.dma_start(
                        out=outf[r * ROUND : (r + 1) * ROUND, lo : lo + width].rearrange(
                            "(p n) d -> p n d", n=TILES
                        )[:, n, :],
                        in_=o_out[r][:, n, lo : lo + width],
                    )
            rows = outf[r * ROUND : (r + 1) * ROUND, :].rearrange("(p n) d -> p n d", n=TILES)
            if r < ROUNDS - 2 and n == TILES - 1:
                nc.sync.dma_start(out=rows, in_=o_out[r][:])

        def vector_sbuf_work(s):
            rs, rems = divmod(s + 27, 8)
            if 0 <= rs < ROUNDS:
                slots = BN_SLOTS[TILES - S_TILES[rs]]
                if rems in slots:
                    bn(rs, slots.index(rems))
            r, rem = divmod(s + 10, 8)
            if rem == 0 and 0 <= r < ROUNDS:
                x_quant(r)
            if s == -23:
                nc.vector.tensor_copy(out=bg_col[:], in_=bg_ps[:, 0:8])
            if s == -19:
                regroup_wg(0)
            if s == -19:
                regroup_wg(1)
            if s == -18:
                quantise_wg(0)
            if s == -10:
                quantise_wg(1)
            if s == -3:
                regroup_wo(0)
            if s == 0:
                regroup_wo(1)
            if s == 2:
                nc.vector.quantize_mx(
                    out=wo_codes[:].bitcast(FP8X4), scales=wo_scales[:], in_=wo_grp[:]
                )

        def scalar_sbuf_work(s):
            if 0 <= s + 4 < SLOTS and (s + 4) % 4 not in G_NORM:
                norm(s + 4)

        def scalar_stats(s):
            rs, rems = divmod(s + 24, 8)
            if 0 <= rs < ROUNDS and S_TILES[rs]:
                for step in range(S_TILES[rs] * rems, S_TILES[rs] * rems + S_TILES[rs]):
                    s_stat(rs, step)

        def scalar_psum_work(s):
            if 0 <= s + 7 < SLOTS:
                gate_act(s + 7)

        def scalar_x_out(s):
            r, rem = divmod(s + 17, 8)
            if 0 <= r < ROUNDS and rem in (0, 4):
                x_out(r, rem // 4)

        for s in range(-34, SLOTS + 10):
            r, rem = divmod(s + 36, 8)
            if rem == 0 and 1 <= r < ROUNDS:
                load_o(r)
            r, rem = divmod(s + 30, 8)
            if rem == 0 and 1 <= r < ROUNDS:
                load_x(r)
            if s == -16:
                nc.sync.dma_start(out=wo_raw[:], in_=Wo.rearrange("(q p) d -> p q d", p=P))
            if s == -6:
                nc.sync.dma_start(out=bo_b[:], in_=bo.partition_broadcast(P))

            r, rem = divmod(s + 15, 8)
            if rem == 0 and 0 <= r < ROUNDS:
                inverse_deviation(r)
            if 0 <= s + 12 < SLOTS and (s + 12) % 4 in G_NORM:
                norm(s + 12)

            if 0 <= s + 2 < SLOTS:
                flip(s + 2)
            r, rem = divmod(s + 18, 8)
            if 0 <= r < ROUNDS and rem in (0, 1, 4, 4 + 1):
                x_flip(r, rem // 4, rem % 4)
            if 0 <= s + 7 < SLOTS:
                gate_mm(s + 7)
            if 0 <= s - 8 < SLOTS:
                out_mm(s - 8)

            if s % 2 == 1:
                scalar_sbuf_work(s - 1)
                scalar_stats(s - 1)
                scalar_psum_work(s - 1)
                scalar_sbuf_work(s)
                scalar_stats(s)
                scalar_psum_work(s)
                scalar_x_out(s - 1)
                scalar_x_out(s)
            else:
                if 0 <= s < SLOTS:
                    prod(s)
                    prod(s + 1)
                if s >= 10 and (s - 10) // 2 < 4 * ROUNDS:
                    out_add((s - 10) // 2)
                if 0 <= s - 2 < SLOTS:
                    h_quant((s - 2) // 4, ((s - 2) % 4) // 2)
                vector_sbuf_work(s)
                vector_sbuf_work(s + 1)
